import numpy as np
import ml_dtypes


def mxq(x, axis, fmt="e4m3"):
    dtype, down = {"e4m3": (ml_dtypes.float8_e4m3fn, 7), "e5m2": (ml_dtypes.float8_e5m2, 14)}[fmt]
    v = np.moveaxis(np.asarray(x, np.float32).astype(ml_dtypes.bfloat16).astype(np.float64), axis, -1)
    blocks = v.reshape(v.shape[:-1] + (-1, 32))
    amax = np.abs(blocks).max(-1, keepdims=True)
    byte = np.maximum(np.where(amax > 0, np.frexp(amax)[1] - 1 + 127, 0) - down, 1)
    scale = np.exp2(byte - 127.0)
    codes = (blocks / scale).astype(np.float32).astype(dtype).astype(np.float64)
    return np.moveaxis((codes * scale).reshape(v.shape), -1, axis)


WIDE = False


def mx_kscale(k):
    if not WIDE:
        return np.ones(k)
    levels = np.array([10, -10, 5, -5, 0])
    a = np.random.permutation(np.resize(levels, k // 512 * 4)).reshape(k // 512, 4)
    idx = np.arange(k)
    return np.exp2(a[idx // 512, idx % 128 // 32])


BF16 = ml_dtypes.bfloat16


def bf(x):
    return np.asarray(x, np.float32).astype(BF16)


def f64(x):
    return np.asarray(x).astype(np.float64)


B, H = 4096, 512
K = 2 * H
BETA_SHIFT = 1.0
LN_EPS = 1e-5
BAG_EPS = 1e-6


def setup_inputs():
    s = mx_kscale(H)
    r_main = np.random.uniform(0.5, 1.1, (B, 1))
    r_branch = np.random.uniform(0.5, 1.1, (B, 1))
    w_mb = np.random.standard_normal((K, H)) / np.sqrt(K)
    w_mb[H:] = w_mb[H:] / s[:, None]
    return {"main": bf(np.random.standard_normal((B, H)) * r_main),
            "branch": bf(np.random.standard_normal((B, H)) * r_branch * s),
            "o": bf(1.0 - np.random.random((B, 1)) * np.random.uniform(0.2, 0.8, (B, H))),
            "is_bag": bf(np.random.random((B, 1))),
            "W_mb": bf(w_mb),
            "b_mb": bf(np.random.standard_normal(H) * 0.3),
            "W_b": bf(np.random.standard_normal((H, H)) * 2.0 / np.sqrt(H) / s[:, None]),
            "b_b": bf(np.random.standard_normal(H) * 0.3),
            "ln_g": bf(1.0 + 0.1 * np.random.standard_normal(H)),
            "ln_b": bf(0.1 * np.random.standard_normal(H))}


def reference(main, branch, o, is_bag, W_mb, b_mb, W_b, b_b, ln_g, ln_b):
    main, is_bag = f64(main), f64(is_bag)
    mbq = mxq(np.concatenate([main, f64(branch)], axis=-1), 1, "e4m3")
    weight_b = np.maximum((mbq @ mxq(f64(W_mb), 0, "e4m3")) + f64(b_mb), 0.0)
    h_m = weight_b * ((mbq[:, H:] @ mxq(f64(W_b), 0, "e4m3")) + f64(b_b))
    em_norm = np.sqrt((main ** 2).sum(-1))
    hm_norm = np.sqrt((h_m ** 2).sum(-1))
    hm_norm = np.where(hm_norm == 0, np.ones_like(hm_norm), hm_norm)
    alpha = np.minimum(em_norm / (hm_norm + BAG_EPS) * BETA_SHIFT, 1.0)[:, None]
    pre = alpha * h_m + main
    mu = pre.mean(-1, keepdims=True)
    var = ((pre - mu) ** 2).mean(-1, keepdims=True)
    emb = (pre - mu) / np.sqrt(var + LN_EPS) * f64(ln_g) + f64(ln_b)
    shift_c = emb * is_bag + main * (1.0 - is_bag)
    h = f64(o) * np.tanh(shift_c)
    return h, shift_c

@@ -1,0 +1,437 @@
+from contextlib import ExitStack
+
+import concourse.masks as masks
+import concourse.mybir as mybir
+
+F32 = mybir.dt.float32
+BF16 = mybir.dt.bfloat16
+U8 = mybir.dt.uint8
+U32 = mybir.dt.uint32
+I32 = mybir.dt.int32
+FP8X4 = mybir.dt.float8_e4m3fn_x4
+ALU = mybir.AluOpType
+ACT = mybir.ActivationFunctionType
+
+P = 128
+B = 4096
+H = 512
+NT = B // P
+TG = 4
+NG = NT // TG
+GB = TG * P
+NHB = H // P
+LN_EPS = 1e-5
+BAG_EPS = 1e-6
+
+FLOPS = 2 * B * (2 * H + H) * H
+
+PERIOD = 11.2
+FIRST = -10000.0
+X_ON_V = 2
+H_ON_V = 6
+SPLIT_ST = 6
+TAB = {
+    "ldm": (-75, 0, 0),
+    "ldb": (-74.99, 0, 0),
+    "ldo": (0.39, 0, 0),
+    "xp": (-59.96, 0.08, 0),
+    "x": (-59.09, 0.08, 0),
+    "qzm": (-52.29, 0, 0),
+    "qzb": (-46.3, 0, 0),
+    "m2": (-28.02, 0.44, 0),
+    "powe": (-25.14, 0, 0),
+    "mm": (-31.76, 1.03, 0),
+    "t1": (-29.32, 1.03, 0),
+    "t2": (-29.24, 1.03, 0),
+    "bk1": (-23.96, 0.01, 0),
+    "q": (-19.86, 0.01, 0),
+    "powa": (-19.82, 0, 0),
+    "als": (-17.92, 0, 0),
+    "dg": (-42.93, 0.12, 0),
+    "rm": (-12.93, 0.12, 0),
+    "w": (-9.91, 0.12, 0),
+    "bk2": (-19.64, 0.75, 0),
+    "pr": (-17.49, 0.75, 0),
+    "mu": (-15.22, 0, 0),
+    "vv": (-7.49, 0.53, 0),
+    "y": (-11.72, 3.52, 0),
+    "ve": (-5.52, 0, 0),
+    "powr": (-5.51, 0, 0),
+    "c1": (-2.11, 0, 0),
+    "sc": (-0.31, 0.88, 0),
+    "stsc": (2.36, 0, 0),
+    "th": (7.63, 5.83, 0),
+    "hh": (9.03, 5.83, 0),
+    "sth": (14.88, 0, 0),
+    "wcp": (-57.17, 0.1, 0),
+    "wcp2": (-50.15, 0, 0),
+    "wqz": (-56.97, 0.1, 0),
+    "wqz2": (-41.52, 0, 0),
+    "sthh": (9.05, 5.83, 0),
+    "stsch": (0.59, 1.77, 0),
+}
+
+
+def tile_bag_lstm_pb_t_kernel(
+    tc, main, branch, o, is_bag, W_mb, b_mb, W_b, b_b, ln_g, ln_b, out_0, out_1
+):
+    nc = tc.nc
+    main_v = main.rearrange("(p j) h -> p j h", j=NT)
+    branch_v = branch.rearrange("(p j) h -> p j h", j=NT)
+    o_v = o.rearrange("(p j) h -> p j h", j=NT)
+    h_v = out_0.rearrange("(p j) h -> p j h", j=NT)
+    sc_v = out_1.rearrange("(p j) h -> p j h", j=NT)
+
+    ops = []
+
+    def at(stamp, fn):
+        ops.append((stamp, len(ops), fn))
+
+    def when(kind, g, i=0):
+        return (PERIOD + TAB[kind][2]) * g + TAB[kind][0] + TAB[kind][1] * i
+
+    with ExitStack() as ctx:
+        const = ctx.enter_context(tc.tile_pool(name="const", bufs=1))
+        inp = ctx.enter_context(tc.tile_pool(name="inp", bufs=1))
+        work = ctx.enter_context(tc.tile_pool(name="work", bufs=2))
+        small = ctx.enter_context(tc.tile_pool(name="small", bufs=3))
+        pconst = ctx.enter_context(tc.psum_pool(name="pconst", bufs=1))
+        pmm = ctx.enter_context(tc.psum_pool(name="pmm", bufs=4))
+        ptr = ctx.enter_context(tc.psum_pool(name="ptr", bufs=3))
+
+        tl = {}
+
+        def stat(key, g):
+            if (key, g) not in tl:
+                tl[(key, g)] = small.tile([P, TG], F32, name=key, tag=key)
+            return tl[(key, g)]
+
+        def big(key, g, nbufs):
+            if (key, g) not in tl:
+                tl[(key, g)] = work.tile([P, TG, H], F32, name=key, tag=key, bufs=nbufs)
+            return tl[(key, g)]
+
+        def rows(g):
+            return slice(g * TG, (g + 1) * TG)
+
+        wraw = const.tile([P, 3, 4, H], BF16, name="wraw")
+        wgrp = const.tile([P, 3, H, 4], BF16, name="wgrp", align_bytes=64)
+        wc = const.tile([P, 3, H], U32, name="wc", align_bytes=64)
+        ws = const.tile([P, 3, H], U8, name="ws", align_bytes=64)
+        warm = const.tile([P, 1], F32, name="warm")
+        ident_f = const.tile([P, P], F32, name="ident_f")
+        ident_b = const.tile([P, P], BF16, name="ident_b")
+        ones_b = const.tile([P, P], BF16, name="ones_b")
+        half = const.tile([P, TG], F32, name="half")
+        mhalf = const.tile([P, TG], F32, name="mhalf")
+        zb = const.tile([P, P], BF16, name="zb")
+        zg = const.tile([P, 2 * H], BF16, name="zg")
+        ib_b = const.tile([P, NT], BF16, name="ib_b")
+        biasT = const.tile([P, 2 * NHB], F32, name="biasT")
+        b_bc = const.tile([P, H], BF16, name="b_bc")
+        ibf = const.tile([P, NT], F32, name="ibf")
+        ef = const.tile([P, NT], F32, name="ef")
+        diag = const.tile([P, NT, P], BF16, name="diag")
+        junk = const.tile([P, H], BF16, name="junk")
+        g_ps = pconst.tile([P, H], F32, name="g_ps")
+
+        def load_w(c):
+            if c < 2:
+                src = W_mb.rearrange("(c u q e) n -> c q u (e n)", c=2, u=2, q=P, e=2)[c]
+            else:
+                src = W_b.rearrange("(u q e) n -> q u (e n)", u=2, q=P, e=2)
+            nc.sync.dma_start(out=wraw[:, c].rearrange("p (u e) n -> p u (e n)", u=2, e=2), in_=src)
+
+        def setup():
+            nc.vector.memset(warm[:], 0.0)
+            nc.scalar.dma_start(out=ib_b[:], in_=is_bag.rearrange("(p j) o -> p (j o)", j=NT))
+            nc.vector.memset(zb[:].bitcast(I32), 0)
+            nc.scalar.dma_start(out=zb[0:4, :], in_=b_mb.rearrange("(r c) -> r c", c=P))
+            nc.scalar.dma_start(out=zb[4:8, :], in_=b_b.rearrange("(r c) -> r c", c=P))
+            nc.vector.memset(zg[:].bitcast(I32), 0)
+            nc.scalar.dma_start(out=zg[0:1, 0:H], in_=ln_g.unsqueeze(0))
+            nc.scalar.dma_start(out=zg[0:1, H : 2 * H], in_=ln_b.unsqueeze(0))
+            nc.scalar.activation(out=warm[:], in_=warm[:], func=ACT.Tanh)
+            masks.make_identity(nc, ident_f[:])
+            masks.make_identity(nc, ident_b[:])
+            nc.vector.memset(ones_b[:], 1.0)
+            nc.vector.memset(half[:], 0.5)
+            nc.vector.memset(mhalf[:], -0.5)
+            nc.vector.tensor_copy(out=ibf[:], in_=ib_b[:])
+            nc.vector.tensor_scalar(
+                out=ef[:], in0=ib_b[:], scalar1=-1.0, scalar2=1.0, op0=ALU.mult, op1=ALU.add
+            )
+
+        def setup2():
+            zbT = ptr.tile([P, P], BF16, name="zbT", tag="tr")
+            nc.tensor.transpose(zbT[:], zb[:], ident_b[:])
+            nc.vector.tensor_copy(out=biasT[:], in_=zbT[:, 0 : 2 * NHB])
+            nc.tensor.matmul(out=g_ps[:], lhsT=ones_b[:], rhs=zg[:, 0:H], start=True, stop=True)
+            b_ps = pmm.tile([P, H], F32, name="b_ps", tag="mm")
+            nc.tensor.matmul(out=b_ps[:], lhsT=ones_b[:], rhs=zg[:, H : 2 * H], start=True, stop=True)
+            nc.vector.tensor_copy(out=b_bc[:], in_=b_ps[:])
+
+        def wcopy(c, eng):
+            dst = wgrp[:, c].rearrange("p (a i) t -> p a t i", i=4)
+            src = wraw[:, c].rearrange("p t (a i) -> p a t i", i=4)
+            if eng == "s":
+                nc.scalar.copy(out=dst, in_=src)
+            else:
+                nc.vector.tensor_copy(out=dst, in_=src)
+
+        def wquant(c):
+            nc.vector.quantize_mx(
+                out=wc[:, c, :].bitcast(FP8X4),
+                scales=ws[:, c, :],
+                in_=wgrp[:, c].rearrange("p n t -> p (n t)"),
+            )
+
+        def ld(key, g, view, nbufs):
+            t = inp.tile([P, TG, H], BF16, name=key, tag=key, bufs=nbufs)
+            tl[(key, g)] = t
+            nc.sync.dma_start(out=t[:], in_=view[:, rows(g), :])
+
+        def xp(g, i):
+            srcw = tl[("mt" if i < 2 else "bt", g)][:].bitcast(F32)
+            bank = ptr.tile([P, 2, 2 * P], F32, name="xp", tag="tr")
+            tl[("xp", g, i)] = bank
+            for tt in range(2):
+                for u in range(2):
+                    nc.tensor.transpose(
+                        bank[:, u, tt * P : (tt + 1) * P],
+                        srcw[:, 2 * (i % 2) + tt, u * P : (u + 1) * P],
+                        ident_f[:],
+                    )
+
+        def x(g, i, eng):
+            key = "grpm" if i < 2 else "grpb"
+            if (key, g) not in tl:
+                tl[(key, g)] = work.tile([P, 4 * GB], BF16, name=key, tag=key, bufs=2, align_bytes=64)
+            grpw = tl[(key, g)][:].bitcast(F32).rearrange("p (r u) -> p r u", u=2)
+            hf = i % 2
+            dst = grpw[:, hf * 2 * P : (hf + 1) * 2 * P, :]
+            src = tl[("xp", g, i)][:].rearrange("p u r -> p r u")
+            if eng == "s":
+                nc.scalar.copy(out=dst, in_=src)
+            else:
+                nc.vector.tensor_copy(out=dst, in_=src)
+
+        def qz(g, key):
+            cd = work.tile([P, GB], U32, name="cd" + key, tag="cd" + key, bufs=3, align_bytes=64)
+            sl = work.tile([P, GB], U8, name="sl" + key, tag="sl" + key, bufs=3, align_bytes=64)
+            nc.vector.quantize_mx(out=cd[:].bitcast(FP8X4), scales=sl[:], in_=tl[("grp" + key, g)][:])
+            tl[("cd" + key, g)] = (cd, sl)
+
+        def m2(g, t):
+            nc.scalar.activation(
+                out=junk[:], in_=tl[("mt", g)][:, t, :], func=ACT.Square,
+                accum_out=stat("ssm", g)[:, t : t + 1],
+            )
+
+        def gpow(dst, src, g, expo):
+            nc.gpsimd.tensor_tensor(out=stat(dst, g)[:], in0=stat(src, g)[:], in1=expo[:], op=ALU.pow)
+
+        def mm(g, hb):
+            mc, ms = tl[("cdm", g)]
+            bc, bs = tl[("cdb", g)]
+            cols = slice(hb * P, (hb + 1) * P)
+            g1 = pmm.tile([P, GB], F32, name="g1", tag="mm")
+            nc.tensor.matmul_mx(
+                out=g1[:], lhsT=wc[:, 0, cols].bitcast(FP8X4), lhsT_scale=ws[:, 0, cols],
+                rhs=mc[:].bitcast(FP8X4), rhs_scale=ms[:], start=True, stop=False,
+            )
+            nc.tensor.matmul_mx(
+                out=g1[:], lhsT=wc[:, 1, cols].bitcast(FP8X4), lhsT_scale=ws[:, 1, cols],
+                rhs=bc[:].bitcast(FP8X4), rhs_scale=bs[:], start=False, stop=True,
+            )
+            g2 = pmm.tile([P, GB], F32, name="g2", tag="mm")
+            nc.tensor.matmul_mx(
+                out=g2[:], lhsT=wc[:, 2, cols].bitcast(FP8X4), lhsT_scale=ws[:, 2, cols],
+                rhs=bc[:].bitcast(FP8X4), rhs_scale=bs[:], start=True, stop=True,
+            )
+            tl[("g1", g, hb)] = g1
+            tl[("g2", g, hb)] = g2
+
+        def t1(g, hb):
+            wbT = work.tile([P, GB], F32, name="wbT", tag="wbT", bufs=3)
+            tl[("wbT", g, hb)] = wbT
+            nc.scalar.activation(
+                out=wbT[:], in_=tl[("g1", g, hb)][:], func=ACT.Relu, bias=biasT[:, hb : hb + 1], scale=1.0
+            )
+
+        def t2(g, hb):
+            nc.vector.scalar_tensor_tensor(
+                out=big("hmT", g, 2)[:, hb, :], in0=tl[("g2", g, hb)][:],
+                scalar=biasT[:, NHB + hb : NHB + hb + 1], in1=tl[("wbT", g, hb)][:],
+                op0=ALU.add, op1=ALU.mult,
+            )
+
+        def bk(g, t, which):
+            hmT = tl[("hmT", g)]
+            hm = ptr.tile([P, H], F32, name="hm", tag="tr")
+            tl[(which, g, t)] = hm
+            for hb in range(NHB):
+                nc.tensor.transpose(
+                    hm[:, hb * P : (hb + 1) * P], hmT[:, hb, t * P : (t + 1) * P], ident_f[:]
+                )
+
+        def q(g, t):
+            nc.scalar.activation(
+                out=junk[:], in_=tl[("bk1", g, t)][:], func=ACT.Square,
+                accum_out=stat("ssh", g)[:, t : t + 1],
+            )
+
+        def als(g):
+            nc.vector.tensor_scalar_add(out=stat("den", g)[:], in0=stat("hn", g)[:], scalar1=BAG_EPS)
+            nc.vector.reciprocal(out=stat("rden", g)[:], in_=stat("den", g)[:])
+            nc.vector.tensor_tensor(
+                out=stat("al", g)[:], in0=stat("rden", g)[:], in1=stat("em", g)[:], op=ALU.mult
+            )
+            nc.vector.tensor_scalar_min(out=stat("alpha", g)[:], in0=stat("al", g)[:], scalar1=1.0)
+
+        def dg(g, t):
+            j = g * TG + t
+            nc.gpsimd.tensor_scalar(
+                out=diag[:, j, :], in0=ident_b[:], scalar1=ibf[:, j : j + 1], scalar2=0.0,
+                op0=ALU.mult, op1=ALU.add,
+            )
+
+        def rm(g, t):
+            rp = pmm.tile([P, H], F32, name="rp", tag="mm")
+            tl[("rp", g, t)] = rp
+            nc.tensor.matmul(out=rp[:], lhsT=diag[:, g * TG + t, :], rhs=b_bc[:], start=True, stop=True)
+
+        def w(g, t):
+            j = g * TG + t
+            nc.vector.scalar_tensor_tensor(
+                out=big("wt", g, 3)[:, t, :], in0=tl[("mt", g)][:, t, :], scalar=ef[:, j : j + 1],
+                in1=tl[("rp", g, t)][:], op0=ALU.mult, op1=ALU.add,
+            )
+
+        def pr(g, t):
+            nc.vector.scalar_tensor_tensor(
+                out=big("pre", g, 2)[:, t, :], in0=tl[("bk2", g, t)][:],
+                scalar=stat("alpha", g)[:, t : t + 1], in1=tl[("mt", g)][:, t, :],
+                op0=ALU.mult, op1=ALU.add, accum_out=stat("sp", g)[:, t : t + 1],
+            )
+
+        def mu(g):
+            nc.vector.tensor_scalar_mul(out=stat("mu", g)[:], in0=stat("sp", g)[:], scalar1=1.0 / H)
+
+        def vv(g, t):
+            nc.scalar.activation(
+                out=junk[:], in_=tl[("pre", g)][:, t, :], func=ACT.Square,
+                bias=stat("mu", g)[:, t : t + 1], scale=-1.0, accum_out=stat("ssc", g)[:, t : t + 1],
+            )
+
+        def y(g, t):
+            nc.vector.scalar_tensor_tensor(
+                out=big("y1", g, 2)[:, t, :], in0=tl[("pre", g)][:, t, :],
+                scalar=stat("mu", g)[:, t : t + 1], in1=g_ps[:], op0=ALU.subtract, op1=ALU.mult,
+            )
+
+        def ve(g):
+            nc.vector.tensor_scalar(
+                out=stat("ve", g)[:], in0=stat("ssc", g)[:], scalar1=1.0 / H, scalar2=LN_EPS,
+                op0=ALU.mult, op1=ALU.add,
+            )
+
+        def c1(g):
+            nc.vector.tensor_tensor(
+                out=stat("c1", g)[:], in0=stat("rstd", g)[:], in1=ibf[:, rows(g)], op=ALU.mult
+            )
+
+        def sc(g, t):
+            wt = tl[("wt", g)]
+            nc.vector.scalar_tensor_tensor(
+                out=wt[:, t, :], in0=tl[("y1", g)][:, t, :], scalar=stat("c1", g)[:, t : t + 1],
+                in1=wt[:, t, :], op0=ALU.mult, op1=ALU.add,
+            )
+
+        def stsc(g):
+            nc.sync.dma_start(out=sc_v[:, rows(g), :], in_=tl[("wt", g)][:])
+
+        def stsch(g, hf):
+            two = slice(2 * hf, 2 * hf + 2)
+            nc.sync.dma_start(
+                out=sc_v[:, g * TG + 2 * hf : g * TG + 2 * hf + 2, :], in_=tl[("wt", g)][:, two, :]
+            )
+
+        def th(g, hf):
+            t = work.tile([P, 2, H], F32, name="th", tag="th", bufs=4)
+            tl[("th", g, hf)] = t
+            nc.scalar.activation(out=t[:], in_=tl[("wt", g)][:, 2 * hf : 2 * hf + 2, :], func=ACT.Tanh)
+
+        def hh(g, hf):
+            t = tl[("th", g, hf)]
+            eng = nc.vector if g >= H_ON_V else nc.gpsimd
+            eng.tensor_tensor(
+                out=t[:], in0=t[:], in1=tl[("ot", g)][:, 2 * hf : 2 * hf + 2, :], op=ALU.mult
+            )
+
+        def sth(g, hf):
+            nc.sync.dma_start(
+                out=h_v[:, g * TG + 2 * hf : g * TG + 2 * hf + 2, :], in_=tl[("th", g, hf)][:]
+            )
+
+        at(FIRST, lambda: ld("mt", 0, main_v, 7))
+        at(FIRST + 1, lambda: ld("bt", 0, branch_v, 3))
+        for c in range(3):
+            at(FIRST + 2 + c, lambda c=c: load_w(c))
+        at(FIRST + 5, setup)
+        at(FIRST + 6, setup2)
+        for c in range(2):
+            at(TAB["wcp"][0] + TAB["wcp"][1] * c, lambda c=c: wcopy(c, "v"))
+            at(TAB["wqz"][0] + TAB["wqz"][1] * c, lambda c=c: wquant(c))
+        at(TAB["wcp2"][0], lambda: wcopy(2, "s"))
+        at(TAB["wqz2"][0], lambda: wquant(2))
+        for g in range(NG):
+            if g > 0:
+                at(when("ldm", g), lambda g=g: ld("mt", g, main_v, 7))
+                at(when("ldb", g), lambda g=g: ld("bt", g, branch_v, 3))
+            at(when("ldo", g), lambda g=g: ld("ot", g, o_v, 4))
+            for i in range(4):
+                at(when("xp", g, i), lambda g=g, i=i: xp(g, i))
+                at(when("x", g, i), lambda g=g, i=i: x(g, i, "v" if g < X_ON_V else "s"))
+            at(when("qzm", g), lambda g=g: qz(g, "m"))
+            at(when("qzb", g), lambda g=g: qz(g, "b"))
+            for i in range(4):
+                at(when("m2", g, i), lambda g=g, i=i: m2(g, i))
+            at(when("powe", g), lambda g=g: gpow("em", "ssm", g, half))
+            for i in range(4):
+                at(when("mm", g, i), lambda g=g, i=i: mm(g, i))
+                at(when("t1", g, i), lambda g=g, i=i: t1(g, i))
+                at(when("t2", g, i), lambda g=g, i=i: t2(g, i))
+            for i in range(4):
+                at(when("bk1", g, i), lambda g=g, i=i: bk(g, i, "bk1"))
+                at(when("q", g, i), lambda g=g, i=i: q(g, i))
+            at(when("powa", g), lambda g=g: gpow("hn", "ssh", g, half))
+            at(when("als", g), lambda g=g: als(g))
+            for i in range(4):
+                at(when("dg", g, i), lambda g=g, i=i: dg(g, i))
+                at(when("rm", g, i), lambda g=g, i=i: rm(g, i))
+                at(when("w", g, i), lambda g=g, i=i: w(g, i))
+                at(when("bk2", g, i), lambda g=g, i=i: bk(g, i, "bk2"))
+                at(when("pr", g, i), lambda g=g, i=i: pr(g, i))
+            at(when("mu", g), lambda g=g: mu(g))
+            for i in range(4):
+                at(when("vv", g, i), lambda g=g, i=i: vv(g, i))
+                at(when("y", g, i), lambda g=g, i=i: y(g, i))
+            at(when("ve", g), lambda g=g: ve(g))
+            at(when("powr", g), lambda g=g: gpow("rstd", "ve", g, mhalf))
+            at(when("c1", g), lambda g=g: c1(g))
+            for i in range(4):
+                at(when("sc", g, i), lambda g=g, i=i: sc(g, i))
+            if g >= SPLIT_ST:
+                for i in range(2):
+                    at(when("stsch", g, i), lambda g=g, i=i: stsch(g, i))
+            else:
+                at(when("stsc", g), lambda g=g: stsc(g))
+            for i in range(2):
+                at(when("th", g, i), lambda g=g, i=i: th(g, i))
+                at(when("hh", g, i), lambda g=g, i=i: hh(g, i))
+                at(when("sthh", g, i), lambda g=g, i=i: sth(g, i))
+
+        ctx.enter_context(tc.manual_schedule())
+        for item in sorted(ops):
+            item[2]()

@@ -25,50 +25,43 @@ BAG_EPS = 1e-6
 
 FLOPS = 2 * B * (2 * H + H) * H
 
-PERIOD = 11.2
+PERIOD = 12.5
 FIRST = -10000.0
-X_ON_V = 2
-H_ON_V = 6
-SPLIT_ST = 6
+X_ON_V = 0
+H_ON_V = 8
 TAB = {
-    "ldm": (-75, 0, 0),
-    "ldb": (-74.99, 0, 0),
-    "ldo": (0.39, 0, 0),
-    "xp": (-59.96, 0.08, 0),
-    "x": (-59.09, 0.08, 0),
-    "qzm": (-52.29, 0, 0),
-    "qzb": (-46.3, 0, 0),
-    "m2": (-28.02, 0.44, 0),
-    "powe": (-25.14, 0, 0),
-    "mm": (-31.76, 1.03, 0),
-    "t1": (-29.32, 1.03, 0),
-    "t2": (-29.24, 1.03, 0),
-    "bk1": (-23.96, 0.01, 0),
-    "q": (-19.86, 0.01, 0),
-    "powa": (-19.82, 0, 0),
-    "als": (-17.92, 0, 0),
-    "dg": (-42.93, 0.12, 0),
-    "rm": (-12.93, 0.12, 0),
-    "w": (-9.91, 0.12, 0),
-    "bk2": (-19.64, 0.75, 0),
-    "pr": (-17.49, 0.75, 0),
-    "mu": (-15.22, 0, 0),
-    "vv": (-7.49, 0.53, 0),
-    "y": (-11.72, 3.52, 0),
-    "ve": (-5.52, 0, 0),
-    "powr": (-5.51, 0, 0),
-    "c1": (-2.11, 0, 0),
-    "sc": (-0.31, 0.88, 0),
-    "stsc": (2.36, 0, 0),
-    "th": (7.63, 5.83, 0),
-    "hh": (9.03, 5.83, 0),
-    "sth": (14.88, 0, 0),
-    "wcp": (-57.17, 0.1, 0),
-    "wcp2": (-50.15, 0, 0),
-    "wqz": (-56.97, 0.1, 0),
-    "wqz2": (-41.52, 0, 0),
-    "sthh": (9.05, 5.83, 0),
-    "stsch": (0.59, 1.77, 0),
+    "ldm": (-97.93, 0, 0),
+    "ldb": (-97.92, 0, 0),
+    "ldo": (-29.29, 0, 0),
+    "xp": (-65.55, 0.12, -0.04),
+    "x": (-64.7, 0.12, -0.04),
+    "qzm": (-62.46, 0, -0.04),
+    "qzb": (-61.32, 0, -0.04),
+    "m2": (-32.94, 0.29, 1.03),
+    "mm": (-33.45, 0.37, -0.16),
+    "t1": (-32.82, 0.37, -0.16),
+    "t2": (-32.29, 0.37, -0.16),
+    "bk1": (-25.47, 0.01, -0.06),
+    "q": (-21.75, 0.01, -0.06),
+    "powa": (-19.65, 0, -0.06),
+    "dg": (-47.6, 0.2, -0.14),
+    "rm": (-17.6, 0.2, -0.14),
+    "w": (-13.51, 0.2, -0.14),
+    "bk2": (-19.32, 0.7, 0),
+    "pr": (-18.27, 0.7, 0),
+    "mu": (-15.08, 0, 0),
+    "vv": (-9.27, 0.69, 0),
+    "y": (-11.26, 3.87, 0),
+    "powr": (-4.86, 0, 0),
+    "sc": (-2.92, 2.56, 0),
+    "stsch": (-0.34, 5.13, 0),
+    "th": (7.42, 7.15, 0),
+    "hh": (9.58, 7.15, 0),
+    "sthh": (9.6, 7.15, 0),
+    "wcp": (-51.13, 0.1, 0),
+    "wcp2": (-53.75, 0, 0),
+    "wqz": (-50.93, 0.1, 0),
+    "wqz2": (-45.49, 0, 0),
 }
 
 
@@ -101,14 +94,9 @@ def tile_bag_lstm_pb_t_kernel(
 
         tl = {}
 
-        def stat(key, g):
+        def stat(key, g, width=TG):
             if (key, g) not in tl:
-                tl[(key, g)] = small.tile([P, TG], F32, name=key, tag=key)
-            return tl[(key, g)]
-
-        def big(key, g, nbufs):
-            if (key, g) not in tl:
-                tl[(key, g)] = work.tile([P, TG, H], F32, name=key, tag=key, bufs=nbufs)
+                tl[(key, g)] = small.tile([P, width], F32, name=key, tag=key)
             return tl[(key, g)]
 
         def rows(g):
@@ -122,8 +110,9 @@ def tile_bag_lstm_pb_t_kernel(
         ident_f = const.tile([P, P], F32, name="ident_f")
         ident_b = const.tile([P, P], BF16, name="ident_b")
         ones_b = const.tile([P, P], BF16, name="ones_b")
-        half = const.tile([P, TG], F32, name="half")
+        half = const.tile([P, 2 * TG], F32, name="half")
         mhalf = const.tile([P, TG], F32, name="mhalf")
+        mone = const.tile([P, TG], F32, name="mone")
         zb = const.tile([P, P], BF16, name="zb")
         zg = const.tile([P, 2 * H], BF16, name="zg")
         ib_b = const.tile([P, NT], BF16, name="ib_b")
@@ -157,6 +146,7 @@ def tile_bag_lstm_pb_t_kernel(
             nc.vector.memset(ones_b[:], 1.0)
             nc.vector.memset(half[:], 0.5)
             nc.vector.memset(mhalf[:], -0.5)
+            nc.vector.memset(mone[:], -1.0)
             nc.vector.tensor_copy(out=ibf[:], in_=ib_b[:])
             nc.vector.tensor_scalar(
                 out=ef[:], in0=ib_b[:], scalar1=-1.0, scalar2=1.0, op0=ALU.mult, op1=ALU.add
@@ -225,11 +215,8 @@ def tile_bag_lstm_pb_t_kernel(
         def m2(g, t):
             nc.scalar.activation(
                 out=junk[:], in_=tl[("mt", g)][:, t, :], func=ACT.Square,
-                accum_out=stat("ssm", g)[:, t : t + 1],
+                accum_out=stat("ss", g, 2 * TG)[:, t : t + 1],
             )
-
-        def gpow(dst, src, g, expo):
-            nc.gpsimd.tensor_tensor(out=stat(dst, g)[:], in0=stat(src, g)[:], in1=expo[:], op=ALU.pow)
 
         def mm(g, hb):
             mc, ms = tl[("cdm", g)]
@@ -260,8 +247,10 @@ def tile_bag_lstm_pb_t_kernel(
             )
 
         def t2(g, hb):
+            if ("hmT", g) not in tl:
+                tl[("hmT", g)] = work.tile([P, NHB, GB], F32, name="hmT", tag="hmT", bufs=2)
             nc.vector.scalar_tensor_tensor(
-                out=big("hmT", g, 2)[:, hb, :], in0=tl[("g2", g, hb)][:],
+                out=tl[("hmT", g)][:, hb, :], in0=tl[("g2", g, hb)][:],
                 scalar=biasT[:, NHB + hb : NHB + hb + 1], in1=tl[("wbT", g, hb)][:],
                 op0=ALU.add, op1=ALU.mult,
             )
@@ -278,16 +267,24 @@ def tile_bag_lstm_pb_t_kernel(
         def q(g, t):
             nc.scalar.activation(
                 out=junk[:], in_=tl[("bk1", g, t)][:], func=ACT.Square,
-                accum_out=stat("ssh", g)[:, t : t + 1],
+                accum_out=stat("ss", g, 2 * TG)[:, TG + t : TG + t + 1],
             )
 
-        def als(g):
-            nc.vector.tensor_scalar_add(out=stat("den", g)[:], in0=stat("hn", g)[:], scalar1=BAG_EPS)
-            nc.vector.reciprocal(out=stat("rden", g)[:], in_=stat("den", g)[:])
-            nc.vector.tensor_tensor(
-                out=stat("al", g)[:], in0=stat("rden", g)[:], in1=stat("em", g)[:], op=ALU.mult
+        def powa(g):
+            rt = stat("rt", g, 2 * TG)
+            nc.gpsimd.tensor_tensor(out=rt[:], in0=stat("ss", g, 2 * TG)[:], in1=half[:], op=ALU.pow)
+            nc.gpsimd.tensor_scalar(
+                out=stat("den", g)[:], in0=rt[:, TG : 2 * TG], scalar1=1.0, scalar2=BAG_EPS,
+                op0=ALU.mult, op1=ALU.add,
             )
-            nc.vector.tensor_scalar_min(out=stat("alpha", g)[:], in0=stat("al", g)[:], scalar1=1.0)
+            nc.gpsimd.tensor_tensor(out=stat("rden", g)[:], in0=stat("den", g)[:], in1=mone[:], op=ALU.pow)
+            nc.gpsimd.tensor_tensor(
+                out=stat("al", g)[:], in0=stat("rden", g)[:], in1=rt[:, 0:TG], op=ALU.mult
+            )
+            nc.gpsimd.tensor_scalar(
+                out=stat("alpha", g)[:], in0=stat("al", g)[:], scalar1=1.0, scalar2=0.0,
+                op0=ALU.min, op1=ALU.max,
+            )
 
         def dg(g, t):
             j = g * TG + t
@@ -303,14 +300,18 @@ def tile_bag_lstm_pb_t_kernel(
 
         def w(g, t):
             j = g * TG + t
+            if ("wt", g, t // 2) not in tl:
+                tl[("wt", g, t // 2)] = work.tile([P, 2, H], F32, name="wt", tag="wt", bufs=6)
             nc.vector.scalar_tensor_tensor(
-                out=big("wt", g, 3)[:, t, :], in0=tl[("mt", g)][:, t, :], scalar=ef[:, j : j + 1],
+                out=tl[("wt", g, t // 2)][:, t % 2, :], in0=tl[("mt", g)][:, t, :], scalar=ef[:, j : j + 1],
                 in1=tl[("rp", g, t)][:], op0=ALU.mult, op1=ALU.add,
             )
 
         def pr(g, t):
+            pre = work.tile([P, H], F32, name="pre", tag="pre", bufs=8)
+            tl[("pre", g, t)] = pre
             nc.vector.scalar_tensor_tensor(
-                out=big("pre", g, 2)[:, t, :], in0=tl[("bk2", g, t)][:],
+                out=pre[:], in0=tl[("bk2", g, t)][:],
                 scalar=stat("alpha", g)[:, t : t + 1], in1=tl[("mt", g)][:, t, :],
                 op0=ALU.mult, op1=ALU.add, accum_out=stat("sp", g)[:, t : t + 1],
             )
@@ -320,47 +321,45 @@ def tile_bag_lstm_pb_t_kernel(
 
         def vv(g, t):
             nc.scalar.activation(
-                out=junk[:], in_=tl[("pre", g)][:, t, :], func=ACT.Square,
+                out=junk[:], in_=tl[("pre", g, t)][:], func=ACT.Square,
                 bias=stat("mu", g)[:, t : t + 1], scale=-1.0, accum_out=stat("ssc", g)[:, t : t + 1],
             )
 
         def y(g, t):
+            y1 = work.tile([P, H], F32, name="y1", tag="y1", bufs=8)
+            tl[("y1", g, t)] = y1
             nc.vector.scalar_tensor_tensor(
-                out=big("y1", g, 2)[:, t, :], in0=tl[("pre", g)][:, t, :],
+                out=y1[:], in0=tl[("pre", g, t)][:],
                 scalar=stat("mu", g)[:, t : t + 1], in1=g_ps[:], op0=ALU.subtract, op1=ALU.mult,
             )
 
-        def ve(g):
-            nc.vector.tensor_scalar(
+        def powr(g):
+            nc.gpsimd.tensor_scalar(
                 out=stat("ve", g)[:], in0=stat("ssc", g)[:], scalar1=1.0 / H, scalar2=LN_EPS,
                 op0=ALU.mult, op1=ALU.add,
             )
-
-        def c1(g):
-            nc.vector.tensor_tensor(
+            nc.gpsimd.tensor_tensor(out=stat("rstd", g)[:], in0=stat("ve", g)[:], in1=mhalf[:], op=ALU.pow)
+            nc.gpsimd.tensor_tensor(
                 out=stat("c1", g)[:], in0=stat("rstd", g)[:], in1=ibf[:, rows(g)], op=ALU.mult
             )
 
         def sc(g, t):
-            wt = tl[("wt", g)]
+            wt = tl[("wt", g, t // 2)]
             nc.vector.scalar_tensor_tensor(
-                out=wt[:, t, :], in0=tl[("y1", g)][:, t, :], scalar=stat("c1", g)[:, t : t + 1],
-                in1=wt[:, t, :], op0=ALU.mult, op1=ALU.add,
+                out=wt[:, t % 2, :], in0=tl[("y1", g, t)][:], scalar=stat("c1", g)[:, t : t + 1],
+                in1=wt[:, t % 2, :], op0=ALU.mult, op1=ALU.add,
             )
 
-        def stsc(g):
-            nc.sync.dma_start(out=sc_v[:, rows(g), :], in_=tl[("wt", g)][:])
+        def two(g, hf):
+            return slice(g * TG + 2 * hf, g * TG + 2 * hf + 2)
 
-        def stsch(g, hf):
-            two = slice(2 * hf, 2 * hf + 2)
-            nc.sync.dma_start(
-                out=sc_v[:, g * TG + 2 * hf : g * TG + 2 * hf + 2, :], in_=tl[("wt", g)][:, two, :]
-            )
+        def stsc(g, hf):
+            nc.sync.dma_start(out=sc_v[:, two(g, hf), :], in_=tl[("wt", g, hf)][:])
 
         def th(g, hf):
             t = work.tile([P, 2, H], F32, name="th", tag="th", bufs=4)
             tl[("th", g, hf)] = t
-            nc.scalar.activation(out=t[:], in_=tl[("wt", g)][:, 2 * hf : 2 * hf + 2, :], func=ACT.Tanh)
+            nc.scalar.activation(out=t[:], in_=tl[("wt", g, hf)][:], func=ACT.Tanh)
 
         def hh(g, hf):
             t = tl[("th", g, hf)]
@@ -370,9 +369,7 @@ def tile_bag_lstm_pb_t_kernel(
             )
 
         def sth(g, hf):
-            nc.sync.dma_start(
-                out=h_v[:, g * TG + 2 * hf : g * TG + 2 * hf + 2, :], in_=tl[("th", g, hf)][:]
-            )
+            nc.sync.dma_start(out=h_v[:, two(g, hf), :], in_=tl[("th", g, hf)][:])
 
         at(FIRST, lambda: ld("mt", 0, main_v, 7))
         at(FIRST + 1, lambda: ld("bt", 0, branch_v, 3))
@@ -382,14 +379,15 @@ def tile_bag_lstm_pb_t_kernel(
         at(FIRST + 6, setup2)
         for c in range(2):
             at(TAB["wcp"][0] + TAB["wcp"][1] * c, lambda c=c: wcopy(c, "v"))
-            at(TAB["wqz"][0] + TAB["wqz"][1] * c, lambda c=c: wquant(c))
         at(TAB["wcp2"][0], lambda: wcopy(2, "s"))
+        for c in range(2):
+            at(TAB["wqz"][0] + TAB["wqz"][1] * c, lambda c=c: wquant(c))
         at(TAB["wqz2"][0], lambda: wquant(2))
         for g in range(NG):
             if g > 0:
                 at(when("ldm", g), lambda g=g: ld("mt", g, main_v, 7))
                 at(when("ldb", g), lambda g=g: ld("bt", g, branch_v, 3))
-            at(when("ldo", g), lambda g=g: ld("ot", g, o_v, 4))
+            at(when("ldo", g), lambda g=g: ld("ot", g, o_v, 3))
             for i in range(4):
                 at(when("xp", g, i), lambda g=g, i=i: xp(g, i))
                 at(when("x", g, i), lambda g=g, i=i: x(g, i, "v" if g < X_ON_V else "s"))
@@ -397,7 +395,6 @@ def tile_bag_lstm_pb_t_kernel(
             at(when("qzb", g), lambda g=g: qz(g, "b"))
             for i in range(4):
                 at(when("m2", g, i), lambda g=g, i=i: m2(g, i))
-            at(when("powe", g), lambda g=g: gpow("em", "ssm", g, half))
             for i in range(4):
                 at(when("mm", g, i), lambda g=g, i=i: mm(g, i))
                 at(when("t1", g, i), lambda g=g, i=i: t1(g, i))
@@ -405,8 +402,7 @@ def tile_bag_lstm_pb_t_kernel(
             for i in range(4):
                 at(when("bk1", g, i), lambda g=g, i=i: bk(g, i, "bk1"))
                 at(when("q", g, i), lambda g=g, i=i: q(g, i))
-            at(when("powa", g), lambda g=g: gpow("hn", "ssh", g, half))
-            at(when("als", g), lambda g=g: als(g))
+            at(when("powa", g), lambda g=g: powa(g))
             for i in range(4):
                 at(when("dg", g, i), lambda g=g, i=i: dg(g, i))
                 at(when("rm", g, i), lambda g=g, i=i: rm(g, i))
@@ -417,17 +413,11 @@ def tile_bag_lstm_pb_t_kernel(
             for i in range(4):
                 at(when("vv", g, i), lambda g=g, i=i: vv(g, i))
                 at(when("y", g, i), lambda g=g, i=i: y(g, i))
-            at(when("ve", g), lambda g=g: ve(g))
-            at(when("powr", g), lambda g=g: gpow("rstd", "ve", g, mhalf))
-            at(when("c1", g), lambda g=g: c1(g))
+            at(when("powr", g), lambda g=g: powr(g))
             for i in range(4):
                 at(when("sc", g, i), lambda g=g, i=i: sc(g, i))
-            if g >= SPLIT_ST:
-                for i in range(2):
-                    at(when("stsch", g, i), lambda g=g, i=i: stsch(g, i))
-            else:
-                at(when("stsc", g), lambda g=g: stsc(g))
             for i in range(2):
+                at(when("stsch", g, i), lambda g=g, i=i: stsc(g, i))
                 at(when("th", g, i), lambda g=g, i=i: th(g, i))
                 at(when("hh", g, i), lambda g=g, i=i: hh(g, i))
                 at(when("sthh", g, i), lambda g=g, i=i: sth(g, i))

@@ -28,40 +28,40 @@ FLOPS = 2 * B * (2 * H + H) * H
 PERIOD = 12.5
 FIRST = -10000.0
 X_ON_V = 0
-H_ON_V = 8
+H_ON_V = 7
 TAB = {
-    "ldm": (-97.93, 0, 0),
-    "ldb": (-97.92, 0, 0),
-    "ldo": (-29.29, 0, 0),
-    "xp": (-65.55, 0.12, -0.04),
-    "x": (-64.7, 0.12, -0.04),
-    "qzm": (-62.46, 0, -0.04),
-    "qzb": (-61.32, 0, -0.04),
-    "m2": (-32.94, 0.29, 1.03),
-    "mm": (-33.45, 0.37, -0.16),
-    "t1": (-32.82, 0.37, -0.16),
-    "t2": (-32.29, 0.37, -0.16),
-    "bk1": (-25.47, 0.01, -0.06),
-    "q": (-21.75, 0.01, -0.06),
-    "powa": (-19.65, 0, -0.06),
-    "dg": (-47.6, 0.2, -0.14),
-    "rm": (-17.6, 0.2, -0.14),
-    "w": (-13.51, 0.2, -0.14),
-    "bk2": (-19.32, 0.7, 0),
-    "pr": (-18.27, 0.7, 0),
-    "mu": (-15.08, 0, 0),
-    "vv": (-9.27, 0.69, 0),
-    "y": (-11.26, 3.87, 0),
-    "powr": (-4.86, 0, 0),
-    "sc": (-2.92, 2.56, 0),
-    "stsch": (-0.34, 5.13, 0),
-    "th": (7.42, 7.15, 0),
-    "hh": (9.58, 7.15, 0),
-    "sthh": (9.6, 7.15, 0),
-    "wcp": (-51.13, 0.1, 0),
-    "wcp2": (-53.75, 0, 0),
-    "wqz": (-50.93, 0.1, 0),
-    "wqz2": (-45.49, 0, 0),
+    "ldm": (-78.17, 0, 0),
+    "ldb": (-78.16, 0, 0),
+    "ldo": (-32.7, 0, 0),
+    "xp": (-63.8, 0.07, -0.04),
+    "x": (-61.61, 0.07, -0.04),
+    "qzm": (-59.28, 0, -0.04),
+    "qzb": (-56.95, 0, -0.04),
+    "m2": (-33.15, 0.66, 0.82),
+    "mm": (-34.23, 0.44, 0.06),
+    "t1": (-33.13, 0.44, 0.06),
+    "t2": (-32.49, 0.44, 0.06),
+    "bk1": (-25.25, 0.01, -0.11),
+    "q": (-21.54, 0.01, -0.11),
+    "powa": (-19.06, 0, -0.11),
+    "dg": (-50.04, 0.43, 0.28),
+    "rm": (-20.04, 0.43, 0.28),
+    "w": (-15.18, 0.43, 0.28),
+    "bk2": (-19.89, 0.56, 0),
+    "pr": (-18.56, 0.56, 0),
+    "mu": (-14.13, 0, 0),
+    "vv": (-8.95, 0.73, 0),
+    "y": (-12.63, 4.69, 0),
+    "powr": (-4.79, 0, 0),
+    "sc": (-2.22, 2.65, 0),
+    "stsch": (0.46, 5.31, 0),
+    "th": (6.95, 6.12, 0),
+    "hh": (10.95, 6.12, 0),
+    "sthh": (10.97, 6.12, 0),
+    "wcp": (-68.35, 0.1, 0),
+    "wcp2": (-75.08, 0, 0),
+    "wqz": (-68.15, 0.1, 0),
+    "wqz2": (-54.43, 0, 0),
 }
 
 
@@ -286,11 +286,11 @@ def tile_bag_lstm_pb_t_kernel(
                 op0=ALU.min, op1=ALU.max,
             )
 
-        def dg(g, t):
-            j = g * TG + t
-            nc.gpsimd.tensor_scalar(
-                out=diag[:, j, :], in0=ident_b[:], scalar1=ibf[:, j : j + 1], scalar2=0.0,
-                op0=ALU.mult, op1=ALU.add,
+        def dgw(k):
+            js = slice(8 * k, 8 * k + 8)
+            nc.gpsimd.tensor_tensor(
+                out=diag[:, js, :], in0=ident_b[:].unsqueeze(1).to_broadcast([P, 8, P]),
+                in1=ib_b[:, js].unsqueeze(2).to_broadcast([P, 8, P]), op=ALU.mult,
             )
 
         def rm(g, t):
@@ -371,15 +371,17 @@ def tile_bag_lstm_pb_t_kernel(
         def sth(g, hf):
             nc.sync.dma_start(out=h_v[:, two(g, hf), :], in_=tl[("th", g, hf)][:])
 
-        at(FIRST, lambda: ld("mt", 0, main_v, 7))
-        at(FIRST + 1, lambda: ld("bt", 0, branch_v, 3))
         for c in range(3):
-            at(FIRST + 2 + c, lambda c=c: load_w(c))
+            at(FIRST + c, lambda c=c: load_w(c))
+        at(FIRST + 3, lambda: ld("mt", 0, main_v, 7))
+        at(FIRST + 4, lambda: ld("bt", 0, branch_v, 3))
         at(FIRST + 5, setup)
         at(FIRST + 6, setup2)
+        for k in range(4):
+            at(FIRST + 1000 + k, lambda k=k: dgw(k))
         for c in range(2):
-            at(TAB["wcp"][0] + TAB["wcp"][1] * c, lambda c=c: wcopy(c, "v"))
-        at(TAB["wcp2"][0], lambda: wcopy(2, "s"))
+            at(TAB["wcp"][0] + TAB["wcp"][1] * c, lambda c=c: wcopy(c, "v" if c == 0 else "s"))
+        at(TAB["wcp2"][0], lambda: wcopy(2, "v"))
         for c in range(2):
             at(TAB["wqz"][0] + TAB["wqz"][1] * c, lambda c=c: wquant(c))
         at(TAB["wqz2"][0], lambda: wquant(2))
@@ -404,7 +406,6 @@ def tile_bag_lstm_pb_t_kernel(
                 at(when("q", g, i), lambda g=g, i=i: q(g, i))
             at(when("powa", g), lambda g=g: powa(g))
             for i in range(4):
-                at(when("dg", g, i), lambda g=g, i=i: dg(g, i))
                 at(when("rm", g, i), lambda g=g, i=i: rm(g, i))
                 at(when("w", g, i), lambda g=g, i=i: w(g, i))
                 at(when("bk2", g, i), lambda g=g, i=i: bk(g, i, "bk2"))

@@ -13,416 +13,389 @@ ALU = mybir.AluOpType
 ACT = mybir.ActivationFunctionType
 
 P = 128
-B = 4096
+ROWS = 4096
 H = 512
-NT = B // P
+TILES = ROWS // P
 TG = 4
-NG = NT // TG
-GB = TG * P
-NHB = H // P
+GROUPS = TILES // TG
+GROUP_ROWS = TG * P
+BLOCKS = H // P
 LN_EPS = 1e-5
 BAG_EPS = 1e-6
 
-FLOPS = 2 * B * (2 * H + H) * H
+FLOPS = 2 * ROWS * (2 * H + H) * H
 
-PERIOD = 12.5
-FIRST = -10000.0
-X_ON_V = 0
-H_ON_V = 7
-TAB = {
-    "ldm": (-78.17, 0, 0),
-    "ldb": (-78.16, 0, 0),
-    "ldo": (-32.7, 0, 0),
-    "xp": (-63.8, 0.07, -0.04),
-    "x": (-61.61, 0.07, -0.04),
-    "qzm": (-59.28, 0, -0.04),
-    "qzb": (-56.95, 0, -0.04),
-    "m2": (-33.15, 0.66, 0.82),
-    "mm": (-34.23, 0.44, 0.06),
-    "t1": (-33.13, 0.44, 0.06),
-    "t2": (-32.49, 0.44, 0.06),
-    "bk1": (-25.25, 0.01, -0.11),
-    "q": (-21.54, 0.01, -0.11),
-    "powa": (-19.06, 0, -0.11),
-    "dg": (-50.04, 0.43, 0.28),
-    "rm": (-20.04, 0.43, 0.28),
-    "w": (-15.18, 0.43, 0.28),
-    "bk2": (-19.89, 0.56, 0),
-    "pr": (-18.56, 0.56, 0),
-    "mu": (-14.13, 0, 0),
-    "vv": (-8.95, 0.73, 0),
-    "y": (-12.63, 4.69, 0),
-    "powr": (-4.79, 0, 0),
-    "sc": (-2.22, 2.65, 0),
-    "stsch": (0.46, 5.31, 0),
-    "th": (6.95, 6.12, 0),
-    "hh": (10.95, 6.12, 0),
-    "sthh": (10.97, 6.12, 0),
-    "wcp": (-68.35, 0.1, 0),
-    "wcp2": (-75.08, 0, 0),
-    "wqz": (-68.15, 0.1, 0),
-    "wqz2": (-54.43, 0, 0),
-}
+LAG_QUANTISE = -2
+LAG_NORM = 1
+LAG_PRE = 2
+LAG_STATS = 3
+LAG_CARRY = 3
+LAG_OUT = 4
+LOAD_AHEAD = 1
 
 
 def tile_bag_lstm_pb_t_kernel(
     tc, main, branch, o, is_bag, W_mb, b_mb, W_b, b_b, ln_g, ln_b, out_0, out_1
 ):
     nc = tc.nc
-    main_v = main.rearrange("(p j) h -> p j h", j=NT)
-    branch_v = branch.rearrange("(p j) h -> p j h", j=NT)
-    o_v = o.rearrange("(p j) h -> p j h", j=NT)
-    h_v = out_0.rearrange("(p j) h -> p j h", j=NT)
-    sc_v = out_1.rearrange("(p j) h -> p j h", j=NT)
-
-    ops = []
-
-    def at(stamp, fn):
-        ops.append((stamp, len(ops), fn))
-
-    def when(kind, g, i=0):
-        return (PERIOD + TAB[kind][2]) * g + TAB[kind][0] + TAB[kind][1] * i
+    main_v = main.rearrange("(p j) h -> p j h", j=TILES)
+    branch_v = branch.rearrange("(p j) h -> p j h", j=TILES)
+    o_v = o.rearrange("(p j) h -> p j h", j=TILES)
+    h_v = out_0.rearrange("(p j) h -> p j h", j=TILES)
+    shift_v = out_1.rearrange("(p j) h -> p j h", j=TILES)
 
     with ExitStack() as ctx:
         const = ctx.enter_context(tc.tile_pool(name="const", bufs=1))
-        inp = ctx.enter_context(tc.tile_pool(name="inp", bufs=1))
-        work = ctx.enter_context(tc.tile_pool(name="work", bufs=2))
+        inputs = ctx.enter_context(tc.tile_pool(name="inputs", bufs=3))
+        work = ctx.enter_context(tc.tile_pool(name="work", bufs=3))
         small = ctx.enter_context(tc.tile_pool(name="small", bufs=3))
-        pconst = ctx.enter_context(tc.psum_pool(name="pconst", bufs=1))
-        pmm = ctx.enter_context(tc.psum_pool(name="pmm", bufs=4))
-        ptr = ctx.enter_context(tc.psum_pool(name="ptr", bufs=3))
+        psum_g = ctx.enter_context(tc.psum_pool(name="psum_g", bufs=1))
+        psum = ctx.enter_context(tc.psum_pool(name="psum", bufs=7))
+        ctx.enter_context(tc.manual_schedule())
 
-        tl = {}
+        live = {}
 
-        def stat(key, g, width=TG):
-            if (key, g) not in tl:
-                tl[(key, g)] = small.tile([P, width], F32, name=key, tag=key)
-            return tl[(key, g)]
+        def bank(shape, dtype=F32):
+            return psum.tile(shape, dtype, name="bank", tag="bank")
 
-        def rows(g):
+        def per_row(name, g, width=TG):
+            if (name, g) not in live:
+                live[(name, g)] = small.tile([P, width], F32, name=name, tag=name)
+            return live[(name, g)]
+
+        def tiles_of(g):
             return slice(g * TG, (g + 1) * TG)
 
-        wraw = const.tile([P, 3, 4, H], BF16, name="wraw")
-        wgrp = const.tile([P, 3, H, 4], BF16, name="wgrp", align_bytes=64)
-        wc = const.tile([P, 3, H], U32, name="wc", align_bytes=64)
-        ws = const.tile([P, 3, H], U8, name="ws", align_bytes=64)
-        warm = const.tile([P, 1], F32, name="warm")
+        def pair_of(g, half):
+            return slice(g * TG + 2 * half, g * TG + 2 * half + 2)
+
+        def exists(g):
+            return 0 <= g < GROUPS
+
+        def load_weights(c):
+            if c < 2:
+                rows = W_mb.rearrange("(c u p e) n -> c p u (e n)", c=2, u=2, p=P, e=2)[c]
+            else:
+                rows = W_b.rearrange("(u p e) n -> p u (e n)", u=2, p=P, e=2)
+            nc.sync.dma_start(out=w_rows[:, c].rearrange("p (u e) n -> p u (e n)", u=2, e=2), in_=rows)
+
+        def load_states(g):
+            if not exists(g):
+                return
+            live[("main", g)] = inputs.tile([P, TG, H], BF16, name="main_t", tag="main", bufs=7)
+            nc.sync.dma_start(out=live[("main", g)][:], in_=main_v[:, tiles_of(g), :])
+            live[("branch", g)] = inputs.tile([P, TG, H], BF16, name="branch_t", tag="branch")
+            nc.sync.dma_start(out=live[("branch", g)][:], in_=branch_v[:, tiles_of(g), :])
+
+        def load_o(g):
+            if not exists(g):
+                return
+            live[("o", g)] = inputs.tile([P, TG, H], BF16, name="o_t", tag="o")
+            nc.sync.dma_start(out=live[("o", g)][:], in_=o_v[:, tiles_of(g), :])
+
+        w_rows = const.tile([P, 3, 4, H], BF16, name="w_rows")
+        w_grouped = const.tile([P, 3, H, 4], BF16, name="w_grouped", align_bytes=64)
+        w_words = const.tile([P, 3, H], U32, name="w_words", align_bytes=64)
+        w_scales = const.tile([P, 3, H], U8, name="w_scales", align_bytes=64)
+        table_warm = const.tile([P, 1], F32, name="table_warm")
         ident_f = const.tile([P, P], F32, name="ident_f")
         ident_b = const.tile([P, P], BF16, name="ident_b")
         ones_b = const.tile([P, P], BF16, name="ones_b")
-        half = const.tile([P, 2 * TG], F32, name="half")
-        mhalf = const.tile([P, TG], F32, name="mhalf")
-        mone = const.tile([P, TG], F32, name="mone")
-        zb = const.tile([P, P], BF16, name="zb")
-        zg = const.tile([P, 2 * H], BF16, name="zg")
-        ib_b = const.tile([P, NT], BF16, name="ib_b")
-        biasT = const.tile([P, 2 * NHB], F32, name="biasT")
-        b_bc = const.tile([P, H], BF16, name="b_bc")
-        ibf = const.tile([P, NT], F32, name="ibf")
-        ef = const.tile([P, NT], F32, name="ef")
-        diag = const.tile([P, NT, P], BF16, name="diag")
-        junk = const.tile([P, H], BF16, name="junk")
-        g_ps = pconst.tile([P, H], F32, name="g_ps")
+        exp_half = const.tile([P, 2 * TG], F32, name="exp_half")
+        exp_minus_half = const.tile([P, TG], F32, name="exp_minus_half")
+        exp_minus_one = const.tile([P, TG], F32, name="exp_minus_one")
+        bias_rows = const.tile([P, P], BF16, name="bias_rows")
+        ln_rows = const.tile([P, 2 * H], BF16, name="ln_rows")
+        bag_b = const.tile([P, TILES], BF16, name="bag_b")
+        bag = const.tile([P, TILES], F32, name="bag")
+        not_bag = const.tile([P, TILES], F32, name="not_bag")
+        bias_cols = const.tile([P, 2 * BLOCKS], F32, name="bias_cols")
+        ln_b_all = const.tile([P, H], BF16, name="ln_b_all")
+        bag_diag = const.tile([P, TILES, P], BF16, name="bag_diag")
+        unread = const.tile([P, H], BF16, name="unread")
+        ln_g_all = psum_g.tile([P, H], F32, name="ln_g_all")
 
-        def load_w(c):
-            if c < 2:
-                src = W_mb.rearrange("(c u q e) n -> c q u (e n)", c=2, u=2, q=P, e=2)[c]
-            else:
-                src = W_b.rearrange("(u q e) n -> q u (e n)", u=2, q=P, e=2)
-            nc.sync.dma_start(out=wraw[:, c].rearrange("p (u e) n -> p u (e n)", u=2, e=2), in_=src)
+        for c in range(3):
+            load_weights(c)
+        for g in range(LOAD_AHEAD):
+            load_states(g)
 
-        def setup():
-            nc.vector.memset(warm[:], 0.0)
-            nc.scalar.dma_start(out=ib_b[:], in_=is_bag.rearrange("(p j) o -> p (j o)", j=NT))
-            nc.vector.memset(zb[:].bitcast(I32), 0)
-            nc.scalar.dma_start(out=zb[0:4, :], in_=b_mb.rearrange("(r c) -> r c", c=P))
-            nc.scalar.dma_start(out=zb[4:8, :], in_=b_b.rearrange("(r c) -> r c", c=P))
-            nc.vector.memset(zg[:].bitcast(I32), 0)
-            nc.scalar.dma_start(out=zg[0:1, 0:H], in_=ln_g.unsqueeze(0))
-            nc.scalar.dma_start(out=zg[0:1, H : 2 * H], in_=ln_b.unsqueeze(0))
-            nc.scalar.activation(out=warm[:], in_=warm[:], func=ACT.Tanh)
-            masks.make_identity(nc, ident_f[:])
-            masks.make_identity(nc, ident_b[:])
-            nc.vector.memset(ones_b[:], 1.0)
-            nc.vector.memset(half[:], 0.5)
-            nc.vector.memset(mhalf[:], -0.5)
-            nc.vector.memset(mone[:], -1.0)
-            nc.vector.tensor_copy(out=ibf[:], in_=ib_b[:])
-            nc.vector.tensor_scalar(
-                out=ef[:], in0=ib_b[:], scalar1=-1.0, scalar2=1.0, op0=ALU.mult, op1=ALU.add
+        nc.vector.memset(table_warm[:], 0.0)
+        nc.scalar.dma_start(out=bag_b[:], in_=is_bag.rearrange("(p j) one -> p (j one)", j=TILES))
+        nc.vector.memset(bias_rows[:].bitcast(I32), 0)
+        nc.scalar.dma_start(out=bias_rows[0:BLOCKS, :], in_=b_mb.rearrange("(r c) -> r c", c=P))
+        nc.scalar.dma_start(out=bias_rows[BLOCKS : 2 * BLOCKS, :], in_=b_b.rearrange("(r c) -> r c", c=P))
+        nc.vector.memset(ln_rows[:].bitcast(I32), 0)
+        nc.scalar.dma_start(out=ln_rows[0:1, 0:H], in_=ln_g.unsqueeze(0))
+        nc.scalar.dma_start(out=ln_rows[0:1, H : 2 * H], in_=ln_b.unsqueeze(0))
+        nc.scalar.activation(out=table_warm[:], in_=table_warm[:], func=ACT.Tanh)
+        masks.make_identity(nc, ident_f[:])
+        masks.make_identity(nc, ident_b[:])
+        nc.vector.memset(ones_b[:], 1.0)
+        nc.vector.memset(exp_half[:], 0.5)
+        nc.vector.memset(exp_minus_half[:], -0.5)
+        nc.vector.memset(exp_minus_one[:], -1.0)
+        nc.vector.tensor_copy(out=bag[:], in_=bag_b[:])
+        nc.vector.tensor_scalar(
+            out=not_bag[:], in0=bag_b[:], scalar1=-1.0, scalar2=1.0, op0=ALU.mult, op1=ALU.add
+        )
+        bias_t = bank([P, P], BF16)
+        nc.tensor.transpose(bias_t[:], bias_rows[:], ident_b[:])
+        nc.vector.tensor_copy(out=bias_cols[:], in_=bias_t[:, 0 : 2 * BLOCKS])
+        nc.tensor.matmul(out=ln_g_all[:], lhsT=ones_b[:], rhs=ln_rows[:, 0:H], start=True, stop=True)
+        ln_b_bank = bank([P, H])
+        nc.tensor.matmul(out=ln_b_bank[:], lhsT=ones_b[:], rhs=ln_rows[:, H : 2 * H], start=True, stop=True)
+        nc.vector.tensor_copy(out=ln_b_all[:], in_=ln_b_bank[:])
+        for first in range(0, TILES, 8):
+            some = slice(first, first + 8)
+            nc.gpsimd.tensor_tensor(
+                out=bag_diag[:, some, :], in0=ident_b[:].unsqueeze(1).to_broadcast([P, 8, P]),
+                in1=bag_b[:, some].unsqueeze(2).to_broadcast([P, 8, P]), op=ALU.mult,
             )
 
-        def setup2():
-            zbT = ptr.tile([P, P], BF16, name="zbT", tag="tr")
-            nc.tensor.transpose(zbT[:], zb[:], ident_b[:])
-            nc.vector.tensor_copy(out=biasT[:], in_=zbT[:, 0 : 2 * NHB])
-            nc.tensor.matmul(out=g_ps[:], lhsT=ones_b[:], rhs=zg[:, 0:H], start=True, stop=True)
-            b_ps = pmm.tile([P, H], F32, name="b_ps", tag="mm")
-            nc.tensor.matmul(out=b_ps[:], lhsT=ones_b[:], rhs=zg[:, H : 2 * H], start=True, stop=True)
-            nc.vector.tensor_copy(out=b_bc[:], in_=b_ps[:])
-
-        def wcopy(c, eng):
-            dst = wgrp[:, c].rearrange("p (a i) t -> p a t i", i=4)
-            src = wraw[:, c].rearrange("p t (a i) -> p a t i", i=4)
-            if eng == "s":
+        def group_weights(c, engine):
+            dst = w_grouped[:, c].rearrange("p (a i) t -> p a t i", i=4)
+            src = w_rows[:, c].rearrange("p t (a i) -> p a t i", i=4)
+            if engine == "scalar":
                 nc.scalar.copy(out=dst, in_=src)
             else:
                 nc.vector.tensor_copy(out=dst, in_=src)
 
-        def wquant(c):
+        def quantise_weights(c):
             nc.vector.quantize_mx(
-                out=wc[:, c, :].bitcast(FP8X4),
-                scales=ws[:, c, :],
-                in_=wgrp[:, c].rearrange("p n t -> p (n t)"),
+                out=w_words[:, c, :].bitcast(FP8X4),
+                scales=w_scales[:, c, :],
+                in_=w_grouped[:, c].rearrange("p n t -> p (n t)"),
             )
 
-        def ld(key, g, view, nbufs):
-            t = inp.tile([P, TG, H], BF16, name=key, tag=key, bufs=nbufs)
-            tl[(key, g)] = t
-            nc.sync.dma_start(out=t[:], in_=view[:, rows(g), :])
+        group_weights(0, "vector")
+        group_weights(1, "scalar")
+        quantise_weights(0)
+        group_weights(2, "vector")
+        quantise_weights(1)
+        quantise_weights(2)
 
-        def xp(g, i):
-            srcw = tl[("mt" if i < 2 else "bt", g)][:].bitcast(F32)
-            bank = ptr.tile([P, 2, 2 * P], F32, name="xp", tag="tr")
-            tl[("xp", g, i)] = bank
-            for tt in range(2):
+        def k_to_partitions(g, i):
+            if not exists(g):
+                return
+            which = "main" if i < 2 else "branch"
+            half = i % 2
+            words = live[(which, g)][:].bitcast(F32)
+            turned = bank([P, 2, 2 * P])
+            for t in range(2):
                 for u in range(2):
                     nc.tensor.transpose(
-                        bank[:, u, tt * P : (tt + 1) * P],
-                        srcw[:, 2 * (i % 2) + tt, u * P : (u + 1) * P],
+                        turned[:, u, t * P : (t + 1) * P],
+                        words[:, 2 * half + t, u * P : (u + 1) * P],
                         ident_f[:],
                     )
+            if half == 0:
+                live[(which + "_k", g)] = work.tile(
+                    [P, 4 * GROUP_ROWS], BF16, name=which + "_k", tag=which + "_k", bufs=2, align_bytes=64
+                )
+            grouped = live[(which + "_k", g)][:].bitcast(F32).rearrange("p (r u) -> p r u", u=2)
+            nc.scalar.copy(
+                out=grouped[:, half * 2 * P : (half + 1) * 2 * P, :],
+                in_=turned[:].rearrange("p u r -> p r u"),
+            )
+            if half == 1:
+                words_q = work.tile([P, GROUP_ROWS], U32, name=which + "_w", tag=which + "_w", align_bytes=64)
+                scales_q = work.tile([P, GROUP_ROWS], U8, name=which + "_s", tag=which + "_s", align_bytes=64)
+                nc.vector.quantize_mx(
+                    out=words_q[:].bitcast(FP8X4), scales=scales_q[:], in_=live[(which + "_k", g)][:]
+                )
+                live[(which + "_q", g)] = (words_q, scales_q)
 
-        def x(g, i, eng):
-            key = "grpm" if i < 2 else "grpb"
-            if (key, g) not in tl:
-                tl[(key, g)] = work.tile([P, 4 * GB], BF16, name=key, tag=key, bufs=2, align_bytes=64)
-            grpw = tl[(key, g)][:].bitcast(F32).rearrange("p (r u) -> p r u", u=2)
-            hf = i % 2
-            dst = grpw[:, hf * 2 * P : (hf + 1) * 2 * P, :]
-            src = tl[("xp", g, i)][:].rearrange("p u r -> p r u")
-            if eng == "s":
-                nc.scalar.copy(out=dst, in_=src)
-            else:
-                nc.vector.tensor_copy(out=dst, in_=src)
+        def gate_sums(g, c):
+            if not exists(g):
+                return
+            main_w, main_s = live[("main_q", g)]
+            branch_w, branch_s = live[("branch_q", g)]
+            cols = slice(c * P, (c + 1) * P)
+            sum_mb = bank([P, GROUP_ROWS])
+            nc.tensor.matmul_mx(
+                out=sum_mb[:], lhsT=w_words[:, 0, cols].bitcast(FP8X4), lhsT_scale=w_scales[:, 0, cols],
+                rhs=main_w[:].bitcast(FP8X4), rhs_scale=main_s[:], start=True, stop=False,
+            )
+            nc.tensor.matmul_mx(
+                out=sum_mb[:], lhsT=w_words[:, 1, cols].bitcast(FP8X4), lhsT_scale=w_scales[:, 1, cols],
+                rhs=branch_w[:].bitcast(FP8X4), rhs_scale=branch_s[:], start=False, stop=True,
+            )
+            sum_b = bank([P, GROUP_ROWS])
+            nc.tensor.matmul_mx(
+                out=sum_b[:], lhsT=w_words[:, 2, cols].bitcast(FP8X4), lhsT_scale=w_scales[:, 2, cols],
+                rhs=branch_w[:].bitcast(FP8X4), rhs_scale=branch_s[:], start=True, stop=True,
+            )
+            live[("sum_mb", g, c)] = sum_mb
+            live[("sum_b", g, c)] = sum_b
 
-        def qz(g, key):
-            cd = work.tile([P, GB], U32, name="cd" + key, tag="cd" + key, bufs=3, align_bytes=64)
-            sl = work.tile([P, GB], U8, name="sl" + key, tag="sl" + key, bufs=3, align_bytes=64)
-            nc.vector.quantize_mx(out=cd[:].bitcast(FP8X4), scales=sl[:], in_=tl[("grp" + key, g)][:])
-            tl[("cd" + key, g)] = (cd, sl)
-
-        def m2(g, t):
+        def gate_relu(g, c):
+            if not exists(g):
+                return
+            weight_b = work.tile([P, GROUP_ROWS], F32, name="weight_b", tag="weight_b")
+            live[("weight_b", g, c)] = weight_b
             nc.scalar.activation(
-                out=junk[:], in_=tl[("mt", g)][:, t, :], func=ACT.Square,
-                accum_out=stat("ss", g, 2 * TG)[:, t : t + 1],
+                out=weight_b[:], in_=live[("sum_mb", g, c)][:], func=ACT.Relu,
+                bias=bias_cols[:, c : c + 1], scale=1.0,
             )
 
-        def mm(g, hb):
-            mc, ms = tl[("cdm", g)]
-            bc, bs = tl[("cdb", g)]
-            cols = slice(hb * P, (hb + 1) * P)
-            g1 = pmm.tile([P, GB], F32, name="g1", tag="mm")
-            nc.tensor.matmul_mx(
-                out=g1[:], lhsT=wc[:, 0, cols].bitcast(FP8X4), lhsT_scale=ws[:, 0, cols],
-                rhs=mc[:].bitcast(FP8X4), rhs_scale=ms[:], start=True, stop=False,
-            )
-            nc.tensor.matmul_mx(
-                out=g1[:], lhsT=wc[:, 1, cols].bitcast(FP8X4), lhsT_scale=ws[:, 1, cols],
-                rhs=bc[:].bitcast(FP8X4), rhs_scale=bs[:], start=False, stop=True,
-            )
-            g2 = pmm.tile([P, GB], F32, name="g2", tag="mm")
-            nc.tensor.matmul_mx(
-                out=g2[:], lhsT=wc[:, 2, cols].bitcast(FP8X4), lhsT_scale=ws[:, 2, cols],
-                rhs=bc[:].bitcast(FP8X4), rhs_scale=bs[:], start=True, stop=True,
-            )
-            tl[("g1", g, hb)] = g1
-            tl[("g2", g, hb)] = g2
-
-        def t1(g, hb):
-            wbT = work.tile([P, GB], F32, name="wbT", tag="wbT", bufs=3)
-            tl[("wbT", g, hb)] = wbT
-            nc.scalar.activation(
-                out=wbT[:], in_=tl[("g1", g, hb)][:], func=ACT.Relu, bias=biasT[:, hb : hb + 1], scale=1.0
-            )
-
-        def t2(g, hb):
-            if ("hmT", g) not in tl:
-                tl[("hmT", g)] = work.tile([P, NHB, GB], F32, name="hmT", tag="hmT", bufs=2)
+        def gate_product(g, c):
+            if not exists(g):
+                return
+            if c == 0:
+                live[("h_m_t", g)] = work.tile([P, BLOCKS, GROUP_ROWS], F32, name="h_m_t", tag="h_m_t")
             nc.vector.scalar_tensor_tensor(
-                out=tl[("hmT", g)][:, hb, :], in0=tl[("g2", g, hb)][:],
-                scalar=biasT[:, NHB + hb : NHB + hb + 1], in1=tl[("wbT", g, hb)][:],
+                out=live[("h_m_t", g)][:, c, :], in0=live[("sum_b", g, c)][:],
+                scalar=bias_cols[:, BLOCKS + c : BLOCKS + c + 1], in1=live[("weight_b", g, c)][:],
                 op0=ALU.add, op1=ALU.mult,
             )
 
-        def bk(g, t, which):
-            hmT = tl[("hmT", g)]
-            hm = ptr.tile([P, H], F32, name="hm", tag="tr")
-            tl[(which, g, t)] = hm
-            for hb in range(NHB):
+        def rows_back(g, t):
+            h_m = bank([P, H])
+            for c in range(BLOCKS):
                 nc.tensor.transpose(
-                    hm[:, hb * P : (hb + 1) * P], hmT[:, hb, t * P : (t + 1) * P], ident_f[:]
+                    h_m[:, c * P : (c + 1) * P], live[("h_m_t", g)][:, c, t * P : (t + 1) * P], ident_f[:]
                 )
+            return h_m
 
-        def q(g, t):
+        def norms(g, t):
+            if not exists(g):
+                return
+            squares = per_row("squares", g, 2 * TG)
+            h_m = rows_back(g, t)
             nc.scalar.activation(
-                out=junk[:], in_=tl[("bk1", g, t)][:], func=ACT.Square,
-                accum_out=stat("ss", g, 2 * TG)[:, TG + t : TG + t + 1],
+                out=unread[:], in_=live[("main", g)][:, t, :], func=ACT.Square,
+                accum_out=squares[:, t : t + 1],
+            )
+            nc.scalar.activation(
+                out=unread[:], in_=h_m[:], func=ACT.Square, accum_out=squares[:, TG + t : TG + t + 1]
             )
 
-        def powa(g):
-            rt = stat("rt", g, 2 * TG)
-            nc.gpsimd.tensor_tensor(out=rt[:], in0=stat("ss", g, 2 * TG)[:], in1=half[:], op=ALU.pow)
+        def alpha(g):
+            if not exists(g):
+                return
+            lengths = per_row("lengths", g, 2 * TG)
+            nc.gpsimd.tensor_tensor(
+                out=lengths[:], in0=per_row("squares", g, 2 * TG)[:], in1=exp_half[:], op=ALU.pow
+            )
             nc.gpsimd.tensor_scalar(
-                out=stat("den", g)[:], in0=rt[:, TG : 2 * TG], scalar1=1.0, scalar2=BAG_EPS,
+                out=per_row("below", g)[:], in0=lengths[:, TG : 2 * TG], scalar1=1.0, scalar2=BAG_EPS,
                 op0=ALU.mult, op1=ALU.add,
             )
-            nc.gpsimd.tensor_tensor(out=stat("rden", g)[:], in0=stat("den", g)[:], in1=mone[:], op=ALU.pow)
             nc.gpsimd.tensor_tensor(
-                out=stat("al", g)[:], in0=stat("rden", g)[:], in1=rt[:, 0:TG], op=ALU.mult
+                out=per_row("inverse", g)[:], in0=per_row("below", g)[:], in1=exp_minus_one[:], op=ALU.pow
+            )
+            nc.gpsimd.tensor_tensor(
+                out=per_row("ratio", g)[:], in0=per_row("inverse", g)[:], in1=lengths[:, 0:TG], op=ALU.mult
             )
             nc.gpsimd.tensor_scalar(
-                out=stat("alpha", g)[:], in0=stat("al", g)[:], scalar1=1.0, scalar2=0.0,
+                out=per_row("alpha", g)[:], in0=per_row("ratio", g)[:], scalar1=1.0, scalar2=0.0,
                 op0=ALU.min, op1=ALU.max,
             )
 
-        def dgw(k):
-            js = slice(8 * k, 8 * k + 8)
-            nc.gpsimd.tensor_tensor(
-                out=diag[:, js, :], in0=ident_b[:].unsqueeze(1).to_broadcast([P, 8, P]),
-                in1=ib_b[:, js].unsqueeze(2).to_broadcast([P, 8, P]), op=ALU.mult,
-            )
-
-        def rm(g, t):
-            rp = pmm.tile([P, H], F32, name="rp", tag="mm")
-            tl[("rp", g, t)] = rp
-            nc.tensor.matmul(out=rp[:], lhsT=diag[:, g * TG + t, :], rhs=b_bc[:], start=True, stop=True)
-
-        def w(g, t):
-            j = g * TG + t
-            if ("wt", g, t // 2) not in tl:
-                tl[("wt", g, t // 2)] = work.tile([P, 2, H], F32, name="wt", tag="wt", bufs=6)
+        def shifted(g, t):
+            if not exists(g):
+                return
+            h_m = rows_back(g, t)
+            pre = work.tile([P, H], F32, name="pre", tag="pre", bufs=6)
+            live[("pre", g, t)] = pre
             nc.vector.scalar_tensor_tensor(
-                out=tl[("wt", g, t // 2)][:, t % 2, :], in0=tl[("mt", g)][:, t, :], scalar=ef[:, j : j + 1],
-                in1=tl[("rp", g, t)][:], op0=ALU.mult, op1=ALU.add,
+                out=pre[:], in0=h_m[:], scalar=per_row("alpha", g)[:, t : t + 1],
+                in1=live[("main", g)][:, t, :], op0=ALU.mult, op1=ALU.add,
+                accum_out=per_row("total", g)[:, t : t + 1],
             )
 
-        def pr(g, t):
-            pre = work.tile([P, H], F32, name="pre", tag="pre", bufs=8)
-            tl[("pre", g, t)] = pre
-            nc.vector.scalar_tensor_tensor(
-                out=pre[:], in0=tl[("bk2", g, t)][:],
-                scalar=stat("alpha", g)[:, t : t + 1], in1=tl[("mt", g)][:, t, :],
-                op0=ALU.mult, op1=ALU.add, accum_out=stat("sp", g)[:, t : t + 1],
-            )
+        def mean(g):
+            if not exists(g):
+                return
+            nc.vector.tensor_scalar_mul(out=per_row("mean", g)[:], in0=per_row("total", g)[:], scalar1=1.0 / H)
 
-        def mu(g):
-            nc.vector.tensor_scalar_mul(out=stat("mu", g)[:], in0=stat("sp", g)[:], scalar1=1.0 / H)
-
-        def vv(g, t):
+        def variance(g, t):
+            if not exists(g):
+                return
             nc.scalar.activation(
-                out=junk[:], in_=tl[("pre", g, t)][:], func=ACT.Square,
-                bias=stat("mu", g)[:, t : t + 1], scale=-1.0, accum_out=stat("ssc", g)[:, t : t + 1],
+                out=unread[:], in_=live[("pre", g, t)][:], func=ACT.Square,
+                bias=per_row("mean", g)[:, t : t + 1], scale=-1.0,
+                accum_out=per_row("spread", g)[:, t : t + 1],
             )
 
-        def y(g, t):
-            y1 = work.tile([P, H], F32, name="y1", tag="y1", bufs=8)
-            tl[("y1", g, t)] = y1
+        def centred(g, t):
+            if not exists(g):
+                return
+            scaled = work.tile([P, H], F32, name="scaled", tag="scaled", bufs=8)
+            live[("scaled", g, t)] = scaled
             nc.vector.scalar_tensor_tensor(
-                out=y1[:], in0=tl[("pre", g, t)][:],
-                scalar=stat("mu", g)[:, t : t + 1], in1=g_ps[:], op0=ALU.subtract, op1=ALU.mult,
+                out=scaled[:], in0=live[("pre", g, t)][:], scalar=per_row("mean", g)[:, t : t + 1],
+                in1=ln_g_all[:], op0=ALU.subtract, op1=ALU.mult,
             )
 
-        def powr(g):
+        def bag_over_std(g):
+            if not exists(g):
+                return
             nc.gpsimd.tensor_scalar(
-                out=stat("ve", g)[:], in0=stat("ssc", g)[:], scalar1=1.0 / H, scalar2=LN_EPS,
+                out=per_row("var", g)[:], in0=per_row("spread", g)[:], scalar1=1.0 / H, scalar2=LN_EPS,
                 op0=ALU.mult, op1=ALU.add,
             )
-            nc.gpsimd.tensor_tensor(out=stat("rstd", g)[:], in0=stat("ve", g)[:], in1=mhalf[:], op=ALU.pow)
             nc.gpsimd.tensor_tensor(
-                out=stat("c1", g)[:], in0=stat("rstd", g)[:], in1=ibf[:, rows(g)], op=ALU.mult
+                out=per_row("rstd", g)[:], in0=per_row("var", g)[:], in1=exp_minus_half[:], op=ALU.pow
+            )
+            nc.gpsimd.tensor_tensor(
+                out=per_row("bag_rstd", g)[:], in0=per_row("rstd", g)[:], in1=bag[:, tiles_of(g)], op=ALU.mult
             )
 
-        def sc(g, t):
-            wt = tl[("wt", g, t // 2)]
+        def carry(g, t):
+            if not exists(g):
+                return
+            j = g * TG + t
+            outer = bank([P, H])
+            nc.tensor.matmul(out=outer[:], lhsT=bag_diag[:, j, :], rhs=ln_b_all[:], start=True, stop=True)
+            if t % 2 == 0:
+                live[("shift_c", g, t // 2)] = work.tile([P, 2, H], F32, name="shift_c", tag="shift_c", bufs=6)
             nc.vector.scalar_tensor_tensor(
-                out=wt[:, t % 2, :], in0=tl[("y1", g, t)][:], scalar=stat("c1", g)[:, t : t + 1],
-                in1=wt[:, t % 2, :], op0=ALU.mult, op1=ALU.add,
+                out=live[("shift_c", g, t // 2)][:, t % 2, :], in0=live[("main", g)][:, t, :],
+                scalar=not_bag[:, j : j + 1], in1=outer[:], op0=ALU.mult, op1=ALU.add,
             )
 
-        def two(g, hf):
-            return slice(g * TG + 2 * hf, g * TG + 2 * hf + 2)
-
-        def stsc(g, hf):
-            nc.sync.dma_start(out=sc_v[:, two(g, hf), :], in_=tl[("wt", g, hf)][:])
-
-        def th(g, hf):
-            t = work.tile([P, 2, H], F32, name="th", tag="th", bufs=4)
-            tl[("th", g, hf)] = t
-            nc.scalar.activation(out=t[:], in_=tl[("wt", g, hf)][:], func=ACT.Tanh)
-
-        def hh(g, hf):
-            t = tl[("th", g, hf)]
-            eng = nc.vector if g >= H_ON_V else nc.gpsimd
-            eng.tensor_tensor(
-                out=t[:], in0=t[:], in1=tl[("ot", g)][:, 2 * hf : 2 * hf + 2, :], op=ALU.mult
+        def blend(g, t):
+            if not exists(g):
+                return
+            shift_c = live[("shift_c", g, t // 2)]
+            nc.vector.scalar_tensor_tensor(
+                out=shift_c[:, t % 2, :], in0=live[("scaled", g, t)][:],
+                scalar=per_row("bag_rstd", g)[:, t : t + 1], in1=shift_c[:, t % 2, :],
+                op0=ALU.mult, op1=ALU.add,
             )
+            if t % 2 == 1:
+                nc.sync.dma_start(out=shift_v[:, pair_of(g, t // 2), :], in_=shift_c[:])
 
-        def sth(g, hf):
-            nc.sync.dma_start(out=h_v[:, two(g, hf), :], in_=tl[("th", g, hf)][:])
+        def gated_tanh(g, half):
+            if not exists(g):
+                return
+            h = work.tile([P, 2, H], F32, name="h", tag="h", bufs=4)
+            nc.scalar.activation(out=h[:], in_=live[("shift_c", g, half)][:], func=ACT.Tanh)
+            nc.gpsimd.tensor_tensor(
+                out=h[:], in0=h[:], in1=live[("o", g)][:, 2 * half : 2 * half + 2, :], op=ALU.mult
+            )
+            nc.sync.dma_start(out=h_v[:, pair_of(g, half), :], in_=h[:])
 
-        for c in range(3):
-            at(FIRST + c, lambda c=c: load_w(c))
-        at(FIRST + 3, lambda: ld("mt", 0, main_v, 7))
-        at(FIRST + 4, lambda: ld("bt", 0, branch_v, 3))
-        at(FIRST + 5, setup)
-        at(FIRST + 6, setup2)
-        for k in range(4):
-            at(FIRST + 1000 + k, lambda k=k: dgw(k))
-        for c in range(2):
-            at(TAB["wcp"][0] + TAB["wcp"][1] * c, lambda c=c: wcopy(c, "v" if c == 0 else "s"))
-        at(TAB["wcp2"][0], lambda: wcopy(2, "v"))
-        for c in range(2):
-            at(TAB["wqz"][0] + TAB["wqz"][1] * c, lambda c=c: wquant(c))
-        at(TAB["wqz2"][0], lambda: wquant(2))
-        for g in range(NG):
-            if g > 0:
-                at(when("ldm", g), lambda g=g: ld("mt", g, main_v, 7))
-                at(when("ldb", g), lambda g=g: ld("bt", g, branch_v, 3))
-            at(when("ldo", g), lambda g=g: ld("ot", g, o_v, 3))
-            for i in range(4):
-                at(when("xp", g, i), lambda g=g, i=i: xp(g, i))
-                at(when("x", g, i), lambda g=g, i=i: x(g, i, "v" if g < X_ON_V else "s"))
-            at(when("qzm", g), lambda g=g: qz(g, "m"))
-            at(when("qzb", g), lambda g=g: qz(g, "b"))
-            for i in range(4):
-                at(when("m2", g, i), lambda g=g, i=i: m2(g, i))
-            for i in range(4):
-                at(when("mm", g, i), lambda g=g, i=i: mm(g, i))
-                at(when("t1", g, i), lambda g=g, i=i: t1(g, i))
-                at(when("t2", g, i), lambda g=g, i=i: t2(g, i))
-            for i in range(4):
-                at(when("bk1", g, i), lambda g=g, i=i: bk(g, i, "bk1"))
-                at(when("q", g, i), lambda g=g, i=i: q(g, i))
-            at(when("powa", g), lambda g=g: powa(g))
-            for i in range(4):
-                at(when("rm", g, i), lambda g=g, i=i: rm(g, i))
-                at(when("w", g, i), lambda g=g, i=i: w(g, i))
-                at(when("bk2", g, i), lambda g=g, i=i: bk(g, i, "bk2"))
-                at(when("pr", g, i), lambda g=g, i=i: pr(g, i))
-            at(when("mu", g), lambda g=g: mu(g))
-            for i in range(4):
-                at(when("vv", g, i), lambda g=g, i=i: vv(g, i))
-                at(when("y", g, i), lambda g=g, i=i: y(g, i))
-            at(when("powr", g), lambda g=g: powr(g))
-            for i in range(4):
-                at(when("sc", g, i), lambda g=g, i=i: sc(g, i))
-            for i in range(2):
-                at(when("stsch", g, i), lambda g=g, i=i: stsc(g, i))
-                at(when("th", g, i), lambda g=g, i=i: th(g, i))
-                at(when("hh", g, i), lambda g=g, i=i: hh(g, i))
-                at(when("sthh", g, i), lambda g=g, i=i: sth(g, i))
-
-        ctx.enter_context(tc.manual_schedule())
-        for item in sorted(ops):
-            item[2]()
+        for r in range(LAG_QUANTISE, GROUPS + LAG_OUT):
+            load_states(r - LAG_QUANTISE + LOAD_AHEAD)
+            load_o(r - LAG_OUT + LOAD_AHEAD)
+            for i in range(TG):
+                gate_sums(r, i)
+                gate_relu(r, i)
+                variance(r - LAG_STATS, i)
+                centred(r - LAG_STATS, i)
+                gate_product(r, i)
+            bag_over_std(r - LAG_STATS)
+            for i in range(TG):
+                norms(r - LAG_NORM, i)
+                shifted(r - LAG_PRE, i)
+                blend(r - LAG_OUT, i)
+            alpha(r - LAG_NORM)
+            mean(r - LAG_PRE)
+            for i in range(TG):
+                carry(r - LAG_CARRY, i)
+                k_to_partitions(r - LAG_QUANTISE, i)
+                if i % 2 == 1:
+                    gated_tanh(r - LAG_OUT, i // 2)

@@ -19,7 +19,7 @@ TILES = ROWS // P
 TG = 4
 GROUPS = TILES // TG
 GROUP_ROWS = TG * P
-BLOCKS = H // P
+CHUNKS = H // P
 LN_EPS = 1e-5
 BAG_EPS = 1e-6
 
@@ -38,11 +38,11 @@ def tile_bag_lstm_pb_t_kernel(
     tc, main, branch, o, is_bag, W_mb, b_mb, W_b, b_b, ln_g, ln_b, out_0, out_1
 ):
     nc = tc.nc
-    main_v = main.rearrange("(p j) h -> p j h", j=TILES)
-    branch_v = branch.rearrange("(p j) h -> p j h", j=TILES)
-    o_v = o.rearrange("(p j) h -> p j h", j=TILES)
-    h_v = out_0.rearrange("(p j) h -> p j h", j=TILES)
-    shift_v = out_1.rearrange("(p j) h -> p j h", j=TILES)
+    main_v = main.rearrange("(p j) col -> p j col", j=TILES)
+    branch_v = branch.rearrange("(p j) col -> p j col", j=TILES)
+    o_v = o.rearrange("(p j) col -> p j col", j=TILES)
+    h_v = out_0.rearrange("(p j) col -> p j col", j=TILES)
+    shift_v = out_1.rearrange("(p j) col -> p j col", j=TILES)
 
     with ExitStack() as ctx:
         const = ctx.enter_context(tc.tile_pool(name="const", bufs=1))
@@ -63,21 +63,24 @@ def tile_bag_lstm_pb_t_kernel(
                 live[(name, g)] = small.tile([P, width], F32, name=name, tag=name)
             return live[(name, g)]
 
+        def unread():
+            return work.tile([P, H], BF16, name="unread", tag="unread", bufs=4)
+
         def tiles_of(g):
             return slice(g * TG, (g + 1) * TG)
 
-        def pair_of(g, half):
+        def two_tiles_of(g, half):
             return slice(g * TG + 2 * half, g * TG + 2 * half + 2)
 
         def exists(g):
             return 0 <= g < GROUPS
 
-        def load_weights(c):
-            if c < 2:
-                rows = W_mb.rearrange("(c u p e) n -> c p u (e n)", c=2, u=2, p=P, e=2)[c]
+        def load_weights(s):
+            if s < 2:
+                rows = W_mb.rearrange("(s u p e) n -> s p u (e n)", s=2, u=2, p=P, e=2)[s]
             else:
                 rows = W_b.rearrange("(u p e) n -> p u (e n)", u=2, p=P, e=2)
-            nc.sync.dma_start(out=w_rows[:, c].rearrange("p (u e) n -> p u (e n)", u=2, e=2), in_=rows)
+            nc.sync.dma_start(out=w_rows[:, s].rearrange("p (u e) n -> p u (e n)", u=2, e=2), in_=rows)
 
         def load_states(g):
             if not exists(g):
@@ -109,22 +112,21 @@ def tile_bag_lstm_pb_t_kernel(
         bag_b = const.tile([P, TILES], BF16, name="bag_b")
         bag = const.tile([P, TILES], F32, name="bag")
         not_bag = const.tile([P, TILES], F32, name="not_bag")
-        bias_cols = const.tile([P, 2 * BLOCKS], F32, name="bias_cols")
+        bias_cols = const.tile([P, 2 * CHUNKS], F32, name="bias_cols")
         ln_b_all = const.tile([P, H], BF16, name="ln_b_all")
         bag_diag = const.tile([P, TILES, P], BF16, name="bag_diag")
-        unread = const.tile([P, H], BF16, name="unread")
         ln_g_all = psum_g.tile([P, H], F32, name="ln_g_all")
 
-        for c in range(3):
-            load_weights(c)
+        for s in range(3):
+            load_weights(s)
         for g in range(LOAD_AHEAD):
             load_states(g)
 
         nc.vector.memset(table_warm[:], 0.0)
         nc.scalar.dma_start(out=bag_b[:], in_=is_bag.rearrange("(p j) one -> p (j one)", j=TILES))
         nc.vector.memset(bias_rows[:].bitcast(I32), 0)
-        nc.scalar.dma_start(out=bias_rows[0:BLOCKS, :], in_=b_mb.rearrange("(r c) -> r c", c=P))
-        nc.scalar.dma_start(out=bias_rows[BLOCKS : 2 * BLOCKS, :], in_=b_b.rearrange("(r c) -> r c", c=P))
+        nc.scalar.dma_start(out=bias_rows[0:CHUNKS, :], in_=b_mb.rearrange("(a x) -> a x", x=P))
+        nc.scalar.dma_start(out=bias_rows[CHUNKS : 2 * CHUNKS, :], in_=b_b.rearrange("(a x) -> a x", x=P))
         nc.vector.memset(ln_rows[:].bitcast(I32), 0)
         nc.scalar.dma_start(out=ln_rows[0:1, 0:H], in_=ln_g.unsqueeze(0))
         nc.scalar.dma_start(out=ln_rows[0:1, H : 2 * H], in_=ln_b.unsqueeze(0))
@@ -141,7 +143,7 @@ def tile_bag_lstm_pb_t_kernel(
         )
         bias_t = bank([P, P], BF16)
         nc.tensor.transpose(bias_t[:], bias_rows[:], ident_b[:])
-        nc.vector.tensor_copy(out=bias_cols[:], in_=bias_t[:, 0 : 2 * BLOCKS])
+        nc.vector.tensor_copy(out=bias_cols[:], in_=bias_t[:, 0 : 2 * CHUNKS])
         nc.tensor.matmul(out=ln_g_all[:], lhsT=ones_b[:], rhs=ln_rows[:, 0:H], start=True, stop=True)
         ln_b_bank = bank([P, H])
         nc.tensor.matmul(out=ln_b_bank[:], lhsT=ones_b[:], rhs=ln_rows[:, H : 2 * H], start=True, stop=True)
@@ -153,19 +155,19 @@ def tile_bag_lstm_pb_t_kernel(
                 in1=bag_b[:, some].unsqueeze(2).to_broadcast([P, 8, P]), op=ALU.mult,
             )
 
-        def group_weights(c, engine):
-            dst = w_grouped[:, c].rearrange("p (a i) t -> p a t i", i=4)
-            src = w_rows[:, c].rearrange("p t (a i) -> p a t i", i=4)
+        def group_weights(s, engine):
+            dst = w_grouped[:, s].rearrange("p (a i) v -> p a v i", i=4)
+            src = w_rows[:, s].rearrange("p v (a i) -> p a v i", i=4)
             if engine == "scalar":
                 nc.scalar.copy(out=dst, in_=src)
             else:
                 nc.vector.tensor_copy(out=dst, in_=src)
 
-        def quantise_weights(c):
+        def quantise_weights(s):
             nc.vector.quantize_mx(
-                out=w_words[:, c, :].bitcast(FP8X4),
-                scales=w_scales[:, c, :],
-                in_=w_grouped[:, c].rearrange("p n t -> p (n t)"),
+                out=w_words[:, s, :].bitcast(FP8X4),
+                scales=w_scales[:, s, :],
+                in_=w_grouped[:, s].rearrange("p n v -> p (n v)"),
             )
 
         group_weights(0, "vector")
@@ -180,23 +182,23 @@ def tile_bag_lstm_pb_t_kernel(
                 return
             which = "main" if i < 2 else "branch"
             half = i % 2
-            words = live[(which, g)][:].bitcast(F32)
+            pairs = live[(which, g)][:].bitcast(F32)
             turned = bank([P, 2, 2 * P])
             for t in range(2):
                 for u in range(2):
                     nc.tensor.transpose(
                         turned[:, u, t * P : (t + 1) * P],
-                        words[:, 2 * half + t, u * P : (u + 1) * P],
+                        pairs[:, 2 * half + t, u * P : (u + 1) * P],
                         ident_f[:],
                     )
             if half == 0:
                 live[(which + "_k", g)] = work.tile(
                     [P, 4 * GROUP_ROWS], BF16, name=which + "_k", tag=which + "_k", bufs=2, align_bytes=64
                 )
-            grouped = live[(which + "_k", g)][:].bitcast(F32).rearrange("p (r u) -> p r u", u=2)
+            grouped = live[(which + "_k", g)][:].bitcast(F32).rearrange("p (row u) -> p row u", u=2)
             nc.scalar.copy(
                 out=grouped[:, half * 2 * P : (half + 1) * 2 * P, :],
-                in_=turned[:].rearrange("p u r -> p r u"),
+                in_=turned[:].rearrange("p u row -> p row u"),
             )
             if half == 1:
                 words_q = work.tile([P, GROUP_ROWS], U32, name=which + "_w", tag=which + "_w", align_bytes=64)
@@ -243,16 +245,16 @@ def tile_bag_lstm_pb_t_kernel(
             if not exists(g):
                 return
             if c == 0:
-                live[("h_m_t", g)] = work.tile([P, BLOCKS, GROUP_ROWS], F32, name="h_m_t", tag="h_m_t")
+                live[("h_m_t", g)] = work.tile([P, CHUNKS, GROUP_ROWS], F32, name="h_m_t", tag="h_m_t")
             nc.vector.scalar_tensor_tensor(
                 out=live[("h_m_t", g)][:, c, :], in0=live[("sum_b", g, c)][:],
-                scalar=bias_cols[:, BLOCKS + c : BLOCKS + c + 1], in1=live[("weight_b", g, c)][:],
+                scalar=bias_cols[:, CHUNKS + c : CHUNKS + c + 1], in1=live[("weight_b", g, c)][:],
                 op0=ALU.add, op1=ALU.mult,
             )
 
         def rows_back(g, t):
             h_m = bank([P, H])
-            for c in range(BLOCKS):
+            for c in range(CHUNKS):
                 nc.tensor.transpose(
                     h_m[:, c * P : (c + 1) * P], live[("h_m_t", g)][:, c, t * P : (t + 1) * P], ident_f[:]
                 )
@@ -264,11 +266,11 @@ def tile_bag_lstm_pb_t_kernel(
             squares = per_row("squares", g, 2 * TG)
             h_m = rows_back(g, t)
             nc.scalar.activation(
-                out=unread[:], in_=live[("main", g)][:, t, :], func=ACT.Square,
+                out=unread()[:], in_=live[("main", g)][:, t, :], func=ACT.Square,
                 accum_out=squares[:, t : t + 1],
             )
             nc.scalar.activation(
-                out=unread[:], in_=h_m[:], func=ACT.Square, accum_out=squares[:, TG + t : TG + t + 1]
+                out=unread()[:], in_=h_m[:], func=ACT.Square, accum_out=squares[:, TG + t : TG + t + 1]
             )
 
         def alpha(g):
@@ -314,7 +316,7 @@ def tile_bag_lstm_pb_t_kernel(
             if not exists(g):
                 return
             nc.scalar.activation(
-                out=unread[:], in_=live[("pre", g, t)][:], func=ACT.Square,
+                out=unread()[:], in_=live[("pre", g, t)][:], func=ACT.Square,
                 bias=per_row("mean", g)[:, t : t + 1], scale=-1.0,
                 accum_out=per_row("spread", g)[:, t : t + 1],
             )
@@ -366,17 +368,18 @@ def tile_bag_lstm_pb_t_kernel(
                 op0=ALU.mult, op1=ALU.add,
             )
             if t % 2 == 1:
-                nc.sync.dma_start(out=shift_v[:, pair_of(g, t // 2), :], in_=shift_c[:])
+                nc.sync.dma_start(out=shift_v[:, two_tiles_of(g, t // 2), :], in_=shift_c[:])
 
         def gated_tanh(g, half):
             if not exists(g):
                 return
             h = work.tile([P, 2, H], F32, name="h", tag="h", bufs=4)
             nc.scalar.activation(out=h[:], in_=live[("shift_c", g, half)][:], func=ACT.Tanh)
-            nc.gpsimd.tensor_tensor(
+            engine = nc.vector if g == GROUPS - 1 else nc.gpsimd
+            engine.tensor_tensor(
                 out=h[:], in0=h[:], in1=live[("o", g)][:, 2 * half : 2 * half + 2, :], op=ALU.mult
             )
-            nc.sync.dma_start(out=h_v[:, pair_of(g, half), :], in_=h[:])
+            nc.sync.dma_start(out=h_v[:, two_tiles_of(g, half), :], in_=h[:])
 
         for r in range(LAG_QUANTISE, GROUPS + LAG_OUT):
             load_states(r - LAG_QUANTISE + LOAD_AHEAD)

@@ -172,10 +172,9 @@ def tile_bag_lstm_pb_t_kernel(
 
         group_weights(0, "vector")
         group_weights(1, "scalar")
-        quantise_weights(0)
         group_weights(2, "vector")
-        quantise_weights(1)
-        quantise_weights(2)
+        for s in range(3):
+            quantise_weights(s)
 
         def k_to_partitions(g, i):
             if not exists(g):
@@ -200,13 +199,16 @@ def tile_bag_lstm_pb_t_kernel(
                 out=grouped[:, half * 2 * P : (half + 1) * 2 * P, :],
                 in_=turned[:].rearrange("p u row -> p row u"),
             )
-            if half == 1:
-                words_q = work.tile([P, GROUP_ROWS], U32, name=which + "_w", tag=which + "_w", align_bytes=64)
-                scales_q = work.tile([P, GROUP_ROWS], U8, name=which + "_s", tag=which + "_s", align_bytes=64)
-                nc.vector.quantize_mx(
-                    out=words_q[:].bitcast(FP8X4), scales=scales_q[:], in_=live[(which + "_k", g)][:]
-                )
-                live[(which + "_q", g)] = (words_q, scales_q)
+
+        def quantise(g, which):
+            if not exists(g):
+                return
+            words_q = work.tile([P, GROUP_ROWS], U32, name=which + "_w", tag=which + "_w", align_bytes=64)
+            scales_q = work.tile([P, GROUP_ROWS], U8, name=which + "_s", tag=which + "_s", align_bytes=64)
+            nc.vector.quantize_mx(
+                out=words_q[:].bitcast(FP8X4), scales=scales_q[:], in_=live[(which + "_k", g)][:]
+            )
+            live[(which + "_q", g)] = (words_q, scales_q)
 
         def gate_sums(g, c):
             if not exists(g):
@@ -242,7 +244,7 @@ def tile_bag_lstm_pb_t_kernel(
             )
 
         def gate_product(g, c):
-            if not exists(g):
+            if not exists(g) or c < 0:
                 return
             if c == 0:
                 live[("h_m_t", g)] = work.tile([P, CHUNKS, GROUP_ROWS], F32, name="h_m_t", tag="h_m_t")
@@ -389,7 +391,8 @@ def tile_bag_lstm_pb_t_kernel(
                 gate_relu(r, i)
                 variance(r - LAG_STATS, i)
                 centred(r - LAG_STATS, i)
-                gate_product(r, i)
+                gate_product(r, i - 1)
+            gate_product(r, TG - 1)
             bag_over_std(r - LAG_STATS)
             for i in range(TG):
                 norms(r - LAG_NORM, i)
@@ -400,5 +403,9 @@ def tile_bag_lstm_pb_t_kernel(
             for i in range(TG):
                 carry(r - LAG_CARRY, i)
                 k_to_partitions(r - LAG_QUANTISE, i)
+                if i == 1:
+                    quantise(r - LAG_QUANTISE - 1, "branch")
+                if i == 3:
+                    quantise(r - LAG_QUANTISE, "main")
                 if i % 2 == 1:
                     gated_tanh(r - LAG_OUT, i // 2)

@@ -195,10 +195,12 @@ def tile_bag_lstm_pb_t_kernel(
                     [P, 4 * GROUP_ROWS], BF16, name=which + "_k", tag=which + "_k", bufs=2, align_bytes=64
                 )
             grouped = live[(which + "_k", g)][:].bitcast(F32).rearrange("p (row u) -> p row u", u=2)
-            nc.scalar.copy(
-                out=grouped[:, half * 2 * P : (half + 1) * 2 * P, :],
-                in_=turned[:].rearrange("p u row -> p row u"),
-            )
+            dst = grouped[:, half * 2 * P : (half + 1) * 2 * P, :]
+            src = turned[:].rearrange("p u row -> p row u")
+            if i == TG - 1:
+                nc.vector.tensor_copy(out=dst, in_=src)
+            else:
+                nc.scalar.copy(out=dst, in_=src)
 
         def quantise(g, which):
             if not exists(g):

from contextlib import ExitStack

import concourse.masks as masks
import concourse.mybir as mybir

F32 = mybir.dt.float32
BF16 = mybir.dt.bfloat16
U8 = mybir.dt.uint8
U32 = mybir.dt.uint32
I32 = mybir.dt.int32
FP8X4 = mybir.dt.float8_e4m3fn_x4
ALU = mybir.AluOpType
ACT = mybir.ActivationFunctionType

P = 128
ROWS = 4096
H = 512
TILES = ROWS // P
TG = 4
GROUPS = TILES // TG
GROUP_ROWS = TG * P
CHUNKS = H // P
LN_EPS = 1e-5
BAG_EPS = 1e-6

FLOPS = 2 * ROWS * (2 * H + H) * H

LAG_QUANTISE = -2
LAG_NORM = 1
LAG_PRE = 2
LAG_STATS = 3
LAG_CARRY = 3
LAG_OUT = 4
LOAD_AHEAD = 1


def tile_bag_lstm_pb_t_kernel(
    tc, main, branch, o, is_bag, W_mb, b_mb, W_b, b_b, ln_g, ln_b, out_0, out_1
):
    nc = tc.nc
    main_v = main.rearrange("(p j) col -> p j col", j=TILES)
    branch_v = branch.rearrange("(p j) col -> p j col", j=TILES)
    o_v = o.rearrange("(p j) col -> p j col", j=TILES)
    h_v = out_0.rearrange("(p j) col -> p j col", j=TILES)
    shift_v = out_1.rearrange("(p j) col -> p j col", j=TILES)

    with ExitStack() as ctx:
        const = ctx.enter_context(tc.tile_pool(name="const", bufs=1))
        inputs = ctx.enter_context(tc.tile_pool(name="inputs", bufs=3))
        work = ctx.enter_context(tc.tile_pool(name="work", bufs=3))
        small = ctx.enter_context(tc.tile_pool(name="small", bufs=3))
        psum_g = ctx.enter_context(tc.psum_pool(name="psum_g", bufs=1))
        psum = ctx.enter_context(tc.psum_pool(name="psum", bufs=7))
        ctx.enter_context(tc.manual_schedule())

        live = {}

        def bank(shape, dtype=F32):
            return psum.tile(shape, dtype, name="bank", tag="bank")

        def per_row(name, g, width=TG):
            if (name, g) not in live:
                live[(name, g)] = small.tile([P, width], F32, name=name, tag=name)
            return live[(name, g)]

        def unread():
            return work.tile([P, H], BF16, name="unread", tag="unread", bufs=4)

        def tiles_of(g):
            return slice(g * TG, (g + 1) * TG)

        def two_tiles_of(g, half):
            return slice(g * TG + 2 * half, g * TG + 2 * half + 2)

        def exists(g):
            return 0 <= g < GROUPS

        def load_weights(s):
            if s < 2:
                rows = W_mb.rearrange("(s u p e) n -> s p u (e n)", s=2, u=2, p=P, e=2)[s]
            else:
                rows = W_b.rearrange("(u p e) n -> p u (e n)", u=2, p=P, e=2)
            nc.sync.dma_start(out=w_rows[:, s].rearrange("p (u e) n -> p u (e n)", u=2, e=2), in_=rows)

        def load_states(g):
            if not exists(g):
                return
            live[("main", g)] = inputs.tile([P, TG, H], BF16, name="main_t", tag="main", bufs=7)
            nc.sync.dma_start(out=live[("main", g)][:], in_=main_v[:, tiles_of(g), :])
            live[("branch", g)] = inputs.tile([P, TG, H], BF16, name="branch_t", tag="branch")
            nc.sync.dma_start(out=live[("branch", g)][:], in_=branch_v[:, tiles_of(g), :])

        def load_o(g):
            if not exists(g):
                return
            live[("o", g)] = inputs.tile([P, TG, H], BF16, name="o_t", tag="o")
            nc.sync.dma_start(out=live[("o", g)][:], in_=o_v[:, tiles_of(g), :])

        w_rows = const.tile([P, 3, 4, H], BF16, name="w_rows")
        w_grouped = const.tile([P, 3, H, 4], BF16, name="w_grouped", align_bytes=64)
        w_words = const.tile([P, 3, H], U32, name="w_words", align_bytes=64)
        w_scales = const.tile([P, 3, H], U8, name="w_scales", align_bytes=64)
        table_warm = const.tile([P, 1], F32, name="table_warm")
        ident_f = const.tile([P, P], F32, name="ident_f")
        ident_b = const.tile([P, P], BF16, name="ident_b")
        ones_b = const.tile([P, P], BF16, name="ones_b")
        exp_half = const.tile([P, 2 * TG], F32, name="exp_half")
        exp_minus_half = const.tile([P, TG], F32, name="exp_minus_half")
        exp_minus_one = const.tile([P, TG], F32, name="exp_minus_one")
        bias_rows = const.tile([P, P], BF16, name="bias_rows")
        ln_rows = const.tile([P, 2 * H], BF16, name="ln_rows")
        bag_b = const.tile([P, TILES], BF16, name="bag_b")
        bag = const.tile([P, TILES], F32, name="bag")
        not_bag = const.tile([P, TILES], F32, name="not_bag")
        bias_cols = const.tile([P, 2 * CHUNKS], F32, name="bias_cols")
        ln_b_all = const.tile([P, H], BF16, name="ln_b_all")
        bag_diag = const.tile([P, TILES, P], BF16, name="bag_diag")
        ln_g_all = psum_g.tile([P, H], F32, name="ln_g_all")

        for s in range(3):
            load_weights(s)
        for g in range(LOAD_AHEAD):
            load_states(g)

        nc.vector.memset(table_warm[:], 0.0)
        nc.scalar.dma_start(out=bag_b[:], in_=is_bag.rearrange("(p j) one -> p (j one)", j=TILES))
        nc.vector.memset(bias_rows[:].bitcast(I32), 0)
        nc.scalar.dma_start(out=bias_rows[0:CHUNKS, :], in_=b_mb.rearrange("(a x) -> a x", x=P))
        nc.scalar.dma_start(out=bias_rows[CHUNKS : 2 * CHUNKS, :], in_=b_b.rearrange("(a x) -> a x", x=P))
        nc.vector.memset(ln_rows[:].bitcast(I32), 0)
        nc.scalar.dma_start(out=ln_rows[0:1, 0:H], in_=ln_g.unsqueeze(0))
        nc.scalar.dma_start(out=ln_rows[0:1, H : 2 * H], in_=ln_b.unsqueeze(0))
        nc.scalar.activation(out=table_warm[:], in_=table_warm[:], func=ACT.Tanh)
        masks.make_identity(nc, ident_f[:])
        masks.make_identity(nc, ident_b[:])
        nc.vector.memset(ones_b[:], 1.0)
        nc.vector.memset(exp_half[:], 0.5)
        nc.vector.memset(exp_minus_half[:], -0.5)
        nc.vector.memset(exp_minus_one[:], -1.0)
        nc.vector.tensor_copy(out=bag[:], in_=bag_b[:])
        nc.vector.tensor_scalar(
            out=not_bag[:], in0=bag_b[:], scalar1=-1.0, scalar2=1.0, op0=ALU.mult, op1=ALU.add
        )
        bias_t = bank([P, P], BF16)
        nc.tensor.transpose(bias_t[:], bias_rows[:], ident_b[:])
        nc.vector.tensor_copy(out=bias_cols[:], in_=bias_t[:, 0 : 2 * CHUNKS])
        nc.tensor.matmul(out=ln_g_all[:], lhsT=ones_b[:], rhs=ln_rows[:, 0:H], start=True, stop=True)
        ln_b_bank = bank([P, H])
        nc.tensor.matmul(out=ln_b_bank[:], lhsT=ones_b[:], rhs=ln_rows[:, H : 2 * H], start=True, stop=True)
        nc.vector.tensor_copy(out=ln_b_all[:], in_=ln_b_bank[:])
        for first in range(0, TILES, 8):
            some = slice(first, first + 8)
            nc.gpsimd.tensor_tensor(
                out=bag_diag[:, some, :], in0=ident_b[:].unsqueeze(1).to_broadcast([P, 8, P]),
                in1=bag_b[:, some].unsqueeze(2).to_broadcast([P, 8, P]), op=ALU.mult,
            )

        def group_weights(s, engine):
            dst = w_grouped[:, s].rearrange("p (a i) v -> p a v i", i=4)
            src = w_rows[:, s].rearrange("p v (a i) -> p a v i", i=4)
            if engine == "scalar":
                nc.scalar.copy(out=dst, in_=src)
            else:
                nc.vector.tensor_copy(out=dst, in_=src)

        def quantise_weights(s):
            nc.vector.quantize_mx(
                out=w_words[:, s, :].bitcast(FP8X4),
                scales=w_scales[:, s, :],
                in_=w_grouped[:, s].rearrange("p n v -> p (n v)"),
            )

        group_weights(0, "vector")
        group_weights(1, "scalar")
        group_weights(2, "vector")
        for s in range(3):
            quantise_weights(s)

        def k_to_partitions(g, i):
            if not exists(g):
                return
            which = "main" if i < 2 else "branch"
            half = i % 2
            pairs = live[(which, g)][:].bitcast(F32)
            turned = bank([P, 2, 2 * P])
            for t in range(2):
                for u in range(2):
                    nc.tensor.transpose(
                        turned[:, u, t * P : (t + 1) * P],
                        pairs[:, 2 * half + t, u * P : (u + 1) * P],
                        ident_f[:],
                    )
            if half == 0:
                live[(which + "_k", g)] = work.tile(
                    [P, 4 * GROUP_ROWS], BF16, name=which + "_k", tag=which + "_k", bufs=2, align_bytes=64
                )
            grouped = live[(which + "_k", g)][:].bitcast(F32).rearrange("p (row u) -> p row u", u=2)
            dst = grouped[:, half * 2 * P : (half + 1) * 2 * P, :]
            src = turned[:].rearrange("p u row -> p row u")
            if i == TG - 1:
                nc.vector.tensor_copy(out=dst, in_=src)
            else:
                nc.scalar.copy(out=dst, in_=src)

        def quantise(g, which):
            if not exists(g):
                return
            words_q = work.tile([P, GROUP_ROWS], U32, name=which + "_w", tag=which + "_w", align_bytes=64)
            scales_q = work.tile([P, GROUP_ROWS], U8, name=which + "_s", tag=which + "_s", align_bytes=64)
            nc.vector.quantize_mx(
                out=words_q[:].bitcast(FP8X4), scales=scales_q[:], in_=live[(which + "_k", g)][:]
            )
            live[(which + "_q", g)] = (words_q, scales_q)

        def gate_sums(g, c):
            if not exists(g):
                return
            main_w, main_s = live[("main_q", g)]
            branch_w, branch_s = live[("branch_q", g)]
            cols = slice(c * P, (c + 1) * P)
            sum_mb = bank([P, GROUP_ROWS])
            nc.tensor.matmul_mx(
                out=sum_mb[:], lhsT=w_words[:, 0, cols].bitcast(FP8X4), lhsT_scale=w_scales[:, 0, cols],
                rhs=main_w[:].bitcast(FP8X4), rhs_scale=main_s[:], start=True, stop=False,
            )
            nc.tensor.matmul_mx(
                out=sum_mb[:], lhsT=w_words[:, 1, cols].bitcast(FP8X4), lhsT_scale=w_scales[:, 1, cols],
                rhs=branch_w[:].bitcast(FP8X4), rhs_scale=branch_s[:], start=False, stop=True,
            )
            sum_b = bank([P, GROUP_ROWS])
            nc.tensor.matmul_mx(
                out=sum_b[:], lhsT=w_words[:, 2, cols].bitcast(FP8X4), lhsT_scale=w_scales[:, 2, cols],
                rhs=branch_w[:].bitcast(FP8X4), rhs_scale=branch_s[:], start=True, stop=True,
            )
            live[("sum_mb", g, c)] = sum_mb
            live[("sum_b", g, c)] = sum_b

        def gate_relu(g, c):
            if not exists(g):
                return
            weight_b = work.tile([P, GROUP_ROWS], F32, name="weight_b", tag="weight_b")
            live[("weight_b", g, c)] = weight_b
            nc.scalar.activation(
                out=weight_b[:], in_=live[("sum_mb", g, c)][:], func=ACT.Relu,
                bias=bias_cols[:, c : c + 1], scale=1.0,
            )

        def gate_product(g, c):
            if not exists(g) or c < 0:
                return
            if c == 0:
                live[("h_m_t", g)] = work.tile([P, CHUNKS, GROUP_ROWS], F32, name="h_m_t", tag="h_m_t")
            nc.vector.scalar_tensor_tensor(
                out=live[("h_m_t", g)][:, c, :], in0=live[("sum_b", g, c)][:],
                scalar=bias_cols[:, CHUNKS + c : CHUNKS + c + 1], in1=live[("weight_b", g, c)][:],
                op0=ALU.add, op1=ALU.mult,
            )

        def rows_back(g, t):
            h_m = bank([P, H])
            for c in range(CHUNKS):
                nc.tensor.transpose(
                    h_m[:, c * P : (c + 1) * P], live[("h_m_t", g)][:, c, t * P : (t + 1) * P], ident_f[:]
                )
            return h_m

        def norms(g, t):
            if not exists(g):
                return
            squares = per_row("squares", g, 2 * TG)
            h_m = rows_back(g, t)
            nc.scalar.activation(
                out=unread()[:], in_=live[("main", g)][:, t, :], func=ACT.Square,
                accum_out=squares[:, t : t + 1],
            )
            nc.scalar.activation(
                out=unread()[:], in_=h_m[:], func=ACT.Square, accum_out=squares[:, TG + t : TG + t + 1]
            )

        def alpha(g):
            if not exists(g):
                return
            lengths = per_row("lengths", g, 2 * TG)
            nc.gpsimd.tensor_tensor(
                out=lengths[:], in0=per_row("squares", g, 2 * TG)[:], in1=exp_half[:], op=ALU.pow
            )
            nc.gpsimd.tensor_scalar(
                out=per_row("below", g)[:], in0=lengths[:, TG : 2 * TG], scalar1=1.0, scalar2=BAG_EPS,
                op0=ALU.mult, op1=ALU.add,
            )
            nc.gpsimd.tensor_tensor(
                out=per_row("inverse", g)[:], in0=per_row("below", g)[:], in1=exp_minus_one[:], op=ALU.pow
            )
            nc.gpsimd.tensor_tensor(
                out=per_row("ratio", g)[:], in0=per_row("inverse", g)[:], in1=lengths[:, 0:TG], op=ALU.mult
            )
            nc.gpsimd.tensor_scalar(
                out=per_row("alpha", g)[:], in0=per_row("ratio", g)[:], scalar1=1.0, scalar2=0.0,
                op0=ALU.min, op1=ALU.max,
            )

        def shifted(g, t):
            if not exists(g):
                return
            h_m = rows_back(g, t)
            pre = work.tile([P, H], F32, name="pre", tag="pre", bufs=6)
            live[("pre", g, t)] = pre
            nc.vector.scalar_tensor_tensor(
                out=pre[:], in0=h_m[:], scalar=per_row("alpha", g)[:, t : t + 1],
                in1=live[("main", g)][:, t, :], op0=ALU.mult, op1=ALU.add,
                accum_out=per_row("total", g)[:, t : t + 1],
            )

        def mean(g):
            if not exists(g):
                return
            nc.vector.tensor_scalar_mul(out=per_row("mean", g)[:], in0=per_row("total", g)[:], scalar1=1.0 / H)

        def variance(g, t):
            if not exists(g):
                return
            nc.scalar.activation(
                out=unread()[:], in_=live[("pre", g, t)][:], func=ACT.Square,
                bias=per_row("mean", g)[:, t : t + 1], scale=-1.0,
                accum_out=per_row("spread", g)[:, t : t + 1],
            )

        def centred(g, t):
            if not exists(g):
                return
            scaled = work.tile([P, H], F32, name="scaled", tag="scaled", bufs=8)
            live[("scaled", g, t)] = scaled
            nc.vector.scalar_tensor_tensor(
                out=scaled[:], in0=live[("pre", g, t)][:], scalar=per_row("mean", g)[:, t : t + 1],
                in1=ln_g_all[:], op0=ALU.subtract, op1=ALU.mult,
            )

        def bag_over_std(g):
            if not exists(g):
                return
            nc.gpsimd.tensor_scalar(
                out=per_row("var", g)[:], in0=per_row("spread", g)[:], scalar1=1.0 / H, scalar2=LN_EPS,
                op0=ALU.mult, op1=ALU.add,
            )
            nc.gpsimd.tensor_tensor(
                out=per_row("rstd", g)[:], in0=per_row("var", g)[:], in1=exp_minus_half[:], op=ALU.pow
            )
            nc.gpsimd.tensor_tensor(
                out=per_row("bag_rstd", g)[:], in0=per_row("rstd", g)[:], in1=bag[:, tiles_of(g)], op=ALU.mult
            )

        def carry(g, t):
            if not exists(g):
                return
            j = g * TG + t
            outer = bank([P, H])
            nc.tensor.matmul(out=outer[:], lhsT=bag_diag[:, j, :], rhs=ln_b_all[:], start=True, stop=True)
            if t % 2 == 0:
                live[("shift_c", g, t // 2)] = work.tile([P, 2, H], F32, name="shift_c", tag="shift_c", bufs=6)
            nc.vector.scalar_tensor_tensor(
                out=live[("shift_c", g, t // 2)][:, t % 2, :], in0=live[("main", g)][:, t, :],
                scalar=not_bag[:, j : j + 1], in1=outer[:], op0=ALU.mult, op1=ALU.add,
            )

        def blend(g, t):
            if not exists(g):
                return
            shift_c = live[("shift_c", g, t // 2)]
            nc.vector.scalar_tensor_tensor(
                out=shift_c[:, t % 2, :], in0=live[("scaled", g, t)][:],
                scalar=per_row("bag_rstd", g)[:, t : t + 1], in1=shift_c[:, t % 2, :],
                op0=ALU.mult, op1=ALU.add,
            )
            if t % 2 == 1:
                nc.sync.dma_start(out=shift_v[:, two_tiles_of(g, t // 2), :], in_=shift_c[:])

        def gated_tanh(g, half):
            if not exists(g):
                return
            h = work.tile([P, 2, H], F32, name="h", tag="h", bufs=4)
            nc.scalar.activation(out=h[:], in_=live[("shift_c", g, half)][:], func=ACT.Tanh)
            engine = nc.vector if g == GROUPS - 1 else nc.gpsimd
            engine.tensor_tensor(
                out=h[:], in0=h[:], in1=live[("o", g)][:, 2 * half : 2 * half + 2, :], op=ALU.mult
            )
            nc.sync.dma_start(out=h_v[:, two_tiles_of(g, half), :], in_=h[:])

        for r in range(LAG_QUANTISE, GROUPS + LAG_OUT):
            load_states(r - LAG_QUANTISE + LOAD_AHEAD)
            load_o(r - LAG_OUT + LOAD_AHEAD)
            for i in range(TG):
                gate_sums(r, i)
                gate_relu(r, i)
                variance(r - LAG_STATS, i)
                centred(r - LAG_STATS, i)
                gate_product(r, i - 1)
            gate_product(r, TG - 1)
            bag_over_std(r - LAG_STATS)
            for i in range(TG):
                norms(r - LAG_NORM, i)
                shifted(r - LAG_PRE, i)
                blend(r - LAG_OUT, i)
            alpha(r - LAG_NORM)
            mean(r - LAG_PRE)
            for i in range(TG):
                carry(r - LAG_CARRY, i)
                k_to_partitions(r - LAG_QUANTISE, i)
                if i == 1:
                    quantise(r - LAG_QUANTISE - 1, "branch")
                if i == 3:
                    quantise(r - LAG_QUANTISE, "main")
                if i % 2 == 1:
                    gated_tanh(r - LAG_OUT, i // 2)
